import numpy as np
import ml_dtypes


def mxq(x, axis, fmt="e4m3"):
    dtype, down = {"e4m3": (ml_dtypes.float8_e4m3fn, 7), "e5m2": (ml_dtypes.float8_e5m2, 14)}[fmt]
    v = np.moveaxis(np.asarray(x, np.float32).astype(ml_dtypes.bfloat16).astype(np.float64), axis, -1)
    blocks = v.reshape(v.shape[:-1] + (-1, 32))
    amax = np.abs(blocks).max(-1, keepdims=True)
    byte = np.maximum(np.where(amax > 0, np.frexp(amax)[1] - 1 + 127, 0) - down, 1)
    scale = np.exp2(byte - 127.0)
    codes = (blocks / scale).astype(np.float32).astype(dtype).astype(np.float64)
    return np.moveaxis((codes * scale).reshape(v.shape), -1, axis)


WIDE = False


def mx_kscale(k):
    if not WIDE:
        return np.ones(k)
    levels = np.array([10, -10, 5, -5, 0])
    a = np.random.permutation(np.resize(levels, k // 512 * 4)).reshape(k // 512, 4)
    idx = np.arange(k)
    return np.exp2(a[idx // 512, idx % 128 // 32])


BF16 = ml_dtypes.bfloat16


def bf(x):
    return np.asarray(x, np.float32).astype(BF16)


def f64(x):
    return np.asarray(x).astype(np.float64)


B, A, E, H, NEXP, NACT = 512, 8, 512, 512, 4, 128
M = B * A


def sigmoid(v):
    return 1.0 / (1.0 + np.exp(-v))


def setup_inputs():
    s, t = mx_kscale(H), mx_kscale(H)
    return {
        "h": bf(np.random.standard_normal((M, H)) * 0.65 * s),
        "gate_logit": bf(np.random.standard_normal((M, NEXP))),
        "e_w1": bf(np.random.standard_normal((NEXP, H, H)) * 1.5 / np.sqrt(H) / s[None, None, :] * t[None, :, None]),
        "e_b1": bf(np.random.standard_normal((NEXP, H)) * 0.3 * t[None, :]),
        "e_w2": bf(np.random.standard_normal((NEXP, NACT, H)) * 2.0 / np.sqrt(H) / t[None, None, :]),
        "e_b2": bf(np.random.standard_normal((NEXP, NACT)) * 0.3),
    }


def reference(h, gate_logit, e_w1, e_b1, e_w2, e_b2):
    hq = mxq(f64(h), 1, "e4m3")
    h1 = np.maximum((hq @ mxq(f64(e_w1), 2, "e4m3").transpose(0, 2, 1)) + f64(e_b1)[:, None, :], 0.0)
    experts_out = (mxq(h1, 2, "e4m3") @ mxq(f64(e_w2), 2, "e4m3").transpose(0, 2, 1)) + f64(e_b2)[:, None, :]
    weight = sigmoid(f64(gate_logit))
    w = weight.T[:, :, None]
    final_q = (experts_out * w).mean(axis=0)
    return final_q, np.swapaxes(experts_out, 0, 1)

@@ -1,0 +1,325 @@
+from contextlib import ExitStack
+
+import concourse.bass as bass
+import concourse.mybir as mybir
+import concourse.tile as tile
+from concourse.masks import make_identity
+
+F32 = mybir.dt.float32
+BF16 = mybir.dt.bfloat16
+U32 = mybir.dt.uint32
+U8 = mybir.dt.uint8
+FP8X4 = mybir.dt.float8_e4m3fn_x4
+ACT = mybir.ActivationFunctionType
+ALU = mybir.AluOpType
+
+P = 128
+M = 4096
+H = 512
+NEXP = 4
+NACT = 128
+R = M // P
+SUB = 4
+NCHUNK = R // SUB
+NSTEP = NCHUNK * NEXP
+
+FLOPS = 2 * M * H * H * NEXP + 2 * M * H * NACT * NEXP
+
+PINNED = True
+V_EXITS = ((0, 2), (0, 3), (1, 2), (1, 3), (2, 2), (2, 3))
+S_REGROUP = ()
+
+
+def tile_mspagent_pb_t_kernel(tc, h, gate_logit, e_w1, e_b1, e_w2, e_b2, out_0, out_1):
+    nc = tc.nc
+    with ExitStack() as ctx:
+        const = ctx.enter_context(tc.tile_pool(name="const", bufs=1))
+        work = ctx.enter_context(tc.tile_pool(name="work", bufs=2))
+        ps_s1 = ctx.enter_context(tc.psum_pool(name="ps_s1", bufs=4))
+        ps_s2 = ctx.enter_context(tc.psum_pool(name="ps_s2", bufs=2))
+        ps_tr = ctx.enter_context(tc.psum_pool(name="ps_tr", bufs=2))
+        if PINNED:
+            ctx.enter_context(tc.manual_schedule())
+
+        h_sb = const.tile([P, R * H], BF16, name="h_sb")
+        w1_sb = const.tile([P, NEXP * 4 * H], BF16, name="w1_sb")
+        w2_sb = const.tile([P, NEXP * H], BF16, name="w2_sb")
+        b1_bf = const.tile([P, NEXP, 4], BF16, name="b1_bf")
+        b1f = const.tile([P, NEXP * 4], F32, name="b1f")
+        b2_bf = const.tile([P, NEXP * NACT], BF16, name="b2_bf")
+        b2f = const.tile([P, NEXP, NACT], F32, name="b2f")
+        g_bf = const.tile([P, R * NEXP], BF16, name="g_bf")
+        g_sig = const.tile([P, R * NEXP], F32, name="g_sig")
+        gq = const.tile([P, R * NEXP], F32, name="gq")
+        ident = const.tile([P, P], F32, name="ident")
+        h_codes = const.tile([P, NCHUNK, 512], U32, name="h_codes", align_bytes=64)
+        h_scales = const.tile([P, NCHUNK, 512], U8, name="h_scales", align_bytes=64)
+        w1_codes = const.tile([P, NEXP, 512], U32, name="w1_codes", align_bytes=64)
+        w1_scales = const.tile([P, NEXP, 512], U8, name="w1_scales", align_bytes=64)
+        w2_codes = const.tile([P, 512], U32, name="w2_codes", align_bytes=64)
+        w2_scales = const.tile([P, 512], U8, name="w2_scales", align_bytes=64)
+
+        h_view = h.rearrange("(p r) k -> p (r k)", r=R)
+        CH = SUB * H
+
+        def load_h(c):
+            nc.sync.dma_start(out=h_sb[:, CH * c : CH * (c + 1)], in_=h_view[:, CH * c : CH * (c + 1)])
+
+        def load_w1(e):
+            nc.sync.dma_start(out=w1_sb[:, 4 * H * e : 4 * H * (e + 1)], in_=e_w1[e].rearrange("(p t) k -> p (t k)", t=4))
+
+        nc.scalar.dma_start(out=g_bf[:], in_=gate_logit.rearrange("(p r) e -> p (r e)", r=R))
+        nc.scalar.dma_start(out=b1_bf[:], in_=e_b1.rearrange("e (p t) -> p e t", t=4))
+        load_h(0)
+        load_w1(0)
+        load_w1(1)
+        load_w1(2)
+        load_w1(3)
+        nc.sync.dma_start(out=w2_sb[:].rearrange("a (e k) -> a e k", e=NEXP), in_=e_w2.rearrange("e a k -> a e k"))
+        load_h(1)
+        nc.scalar.dma_start(out=b2_bf[:], in_=e_b2.rearrange("e a -> (e a)").partition_broadcast(P))
+        for c in range(2, NCHUNK):
+            load_h(c)
+
+        make_identity(nc, ident[:])
+        nc.scalar.activation(out=g_sig[:], in_=g_bf[:], func=ACT.Sigmoid)
+
+        HW = H // 2
+        h_words = h_sb[:].bitcast(F32)
+        w1_words = w1_sb[:].bitcast(F32)
+        w2_words = w2_sb[:].bitcast(F32).rearrange("a (e p u) -> a e u p", e=NEXP, u=2)
+
+        def src_h(c):
+            return lambda j, u: h_words[:, HW * (SUB * c + j) + P * u : HW * (SUB * c + j) + P * (u + 1)]
+
+        def src_w1(e):
+            return lambda j, u: w1_words[:, HW * (4 * e + j) + P * u : HW * (4 * e + j) + P * (u + 1)]
+
+        def src_w2():
+            return lambda j, u: w2_words[:, j, u, :]
+
+        banks = {}
+        grouped = {}
+
+        def prep_t(key, src, pool):
+            for b in range(2):
+                tr = pool.tile([P, 2, 2, P], F32, name="tr", tag="bank")
+                for j in range(2):
+                    for u in range(2):
+                        nc.tensor.transpose(tr[:, j, u, :], src(2 * b + j, u), ident[:])
+                banks[(key, b)] = tr
+
+        def prep_x(key, b, eng):
+            if b == 0:
+                grouped[key] = work.tile([P, 4 * P * 4], BF16, name="gp", tag="gp", bufs=3, align_bytes=64)
+            dst = grouped[key][:].bitcast(F32)[:, 512 * b : 512 * (b + 1)].rearrange("p (j c u) -> p j c u", j=2, u=2)
+            src = banks[(key, b)][:].rearrange("p j u c -> p j c u")
+            if eng == "S":
+                nc.scalar.copy(out=dst, in_=src)
+            else:
+                nc.vector.tensor_copy(out=dst, in_=src)
+
+        def prep_q(key, codes, scales):
+            nc.vector.quantize_mx(
+                out=codes.bitcast(FP8X4),
+                scales=scales,
+                in_=grouped[key][:],
+            )
+
+        def q_h(c):
+            prep_q(("h", c), h_codes[:, c, :], h_scales[:, c, :])
+
+        def q_w1(e):
+            prep_q(("w1", e), w1_codes[:, e, :], w1_scales[:, e, :])
+
+        acc = {}
+        planar = {}
+        inter = {}
+        codes1 = {}
+        acc2 = {}
+        ytile = {}
+        qtile = {}
+
+        def stage1(i, t):
+            c, e = divmod(i, NEXP)
+            a = ps_s1.tile([P, 512], F32, name="acc", tag="bank")
+            nc.tensor.matmul_mx(
+                out=a[:],
+                lhsT=w1_codes[:, e, P * t : P * (t + 1)].bitcast(FP8X4),
+                lhsT_scale=w1_scales[:, e, P * t : P * (t + 1)],
+                rhs=h_codes[:, c, :].bitcast(FP8X4),
+                rhs_scale=h_scales[:, c, :],
+                start=True,
+                stop=True,
+            )
+            acc[(i, t)] = a
+
+        def exit1(i, t):
+            e = i % NEXP
+            if t == 0:
+                planar[i] = work.tile([P, 4, 512], BF16, name="planar", tag="planar", bufs=3)
+            bias = b1f[:, 4 * e + t : 4 * e + t + 1]
+            if (i, t) in V_EXITS:
+                nc.vector.tensor_scalar(
+                    out=planar[i][:, t, :], in0=acc[(i, t)][:], scalar1=bias, scalar2=0.0, op0=ALU.add, op1=ALU.max
+                )
+            else:
+                nc.scalar.activation(out=planar[i][:, t, :], in_=acc[(i, t)][:], func=ACT.Relu, bias=bias, scale=1.0)
+
+        def regroup(i):
+            g = work.tile([P, 512, 4], BF16, name="inter", tag="inter", bufs=2, align_bytes=64)
+            dst = g[:].rearrange("p (c i) t -> p c t i", i=4)
+            src = planar[i][:].rearrange("p t (c i) -> p c t i", i=4)
+            if i in S_REGROUP:
+                nc.scalar.copy(out=dst, in_=src)
+            else:
+                nc.vector.tensor_copy(out=dst, in_=src)
+            inter[i] = g
+
+        def quant1(i):
+            cd = work.tile([P, 512], U32, name="cd1", tag="cd1", bufs=4, align_bytes=64)
+            sc = work.tile([P, 512], U8, name="sc1", tag="sc1", bufs=4, align_bytes=64)
+            nc.vector.quantize_mx(out=cd[:].bitcast(FP8X4), scales=sc[:], in_=inter[i][:].rearrange("p c t -> p (c t)"))
+            codes1[i] = (cd, sc)
+
+        def stage2(i):
+            e = i % NEXP
+            cd, sc = codes1[i]
+            a2 = ps_s2.tile([P, SUB, NACT], F32, name="acc2", tag="bank")
+            for s in range(SUB):
+                nc.tensor.matmul_mx(
+                    out=a2[:, s, :],
+                    lhsT=cd[:, P * s : P * (s + 1)].bitcast(FP8X4),
+                    lhsT_scale=sc[:, P * s : P * (s + 1)],
+                    rhs=w2_codes[:, NACT * e : NACT * (e + 1)].bitcast(FP8X4),
+                    rhs_scale=w2_scales[:, NACT * e : NACT * (e + 1)],
+                    start=True,
+                    stop=True,
+                )
+            acc2[i] = a2
+
+        def y_exit(i):
+            c, e = divmod(i, NEXP)
+            if e == 0:
+                ytile[c] = work.tile([P, SUB, NEXP, NACT], F32, name="y", tag="y", bufs=3)
+            nc.vector.tensor_tensor(
+                out=ytile[c][:, :, e, :],
+                in0=acc2[i][:],
+                in1=b2f[:, e, :].unsqueeze(1).to_broadcast([P, SUB, NACT]),
+                op=ALU.add,
+            )
+
+        def gate_acc(i):
+            c, e = divmod(i, NEXP)
+            if e == 0:
+                qtile[c] = work.tile([P, SUB, NACT], F32, name="q", tag="q", bufs=3)
+            for s in range(SUB):
+                col = (SUB * c + s) * NEXP + e
+                if e == 0:
+                    nc.vector.tensor_scalar(
+                        out=qtile[c][:, s, :], in0=ytile[c][:, s, e, :], scalar1=gq[:, col : col + 1], scalar2=None, op0=ALU.mult
+                    )
+                else:
+                    nc.vector.scalar_tensor_tensor(
+                        out=qtile[c][:, s, :],
+                        in0=ytile[c][:, s, e, :],
+                        scalar=gq[:, col : col + 1],
+                        in1=qtile[c][:, s, :],
+                        op0=ALU.mult,
+                        op1=ALU.add,
+                    )
+
+        out1_view = out_1.rearrange("(p r) e a -> p r (e a)", r=R)
+        out0_view = out_0.rearrange("(p r) a -> p r a", r=R)
+
+        def store_y(c):
+            nc.sync.dma_start(out=out1_view[:, SUB * c : SUB * (c + 1), :], in_=ytile[c][:].rearrange("p s e a -> p s (e a)"))
+
+        def store_q(c):
+            nc.sync.dma_start(out=out0_view[:, SUB * c : SUB * (c + 1), :], in_=qtile[c][:])
+
+        prep_t(("h", 0), src_h(0), ps_tr)
+        prep_x(("h", 0), 0, "S")
+        prep_x(("h", 0), 1, "V")
+        prep_t(("w1", 0), src_w1(0), ps_s2)
+        q_h(0)
+        prep_x(("w1", 0), 0, "S")
+        prep_x(("w1", 0), 1, "V")
+        prep_t(("w1", 1), src_w1(1), ps_tr)
+        nc.vector.tensor_copy(out=b1f[:], in_=b1_bf[:].rearrange("p e t -> p (e t)"))
+        q_w1(0)
+        prep_x(("w1", 1), 0, "S")
+        prep_x(("w1", 1), 1, "S")
+        for t in range(4):
+            stage1(0, t)
+        prep_t(("w1", 2), src_w1(2), ps_s2)
+        q_w1(1)
+
+        def due(i):
+            if i < 3:
+                return []
+            if i == 3:
+                return [0, 1]
+            if i == 4:
+                return [2, 3]
+            return [i - 1]
+
+        for i in range(NSTEP + 1):
+            c, e = divmod(i, NEXP)
+            if i < NSTEP:
+                for t in range(4):
+                    exit1(i, t)
+                    if i + 1 < NSTEP:
+                        stage1(i + 1, t)
+                if i in S_REGROUP:
+                    regroup(i)
+            for j in due(i):
+                stage2(j)
+            if i == 0:
+                prep_t(("w1", 3), src_w1(3), ps_tr)
+            if i == 1:
+                prep_t(("w2", 0), src_w2(), ps_s2)
+                prep_t(("h", 1), src_h(1), ps_tr)
+            if i >= 4 and e == 0 and c + 1 < NCHUNK:
+                prep_t(("h", c + 1), src_h(c + 1), ps_tr)
+            if i == 0:
+                prep_x(("w1", 2), 0, "S")
+                prep_x(("w1", 2), 1, "S")
+            if i == 1:
+                prep_x(("w1", 3), 0, "S")
+                prep_x(("w1", 3), 1, "S")
+            if i == 2:
+                prep_x(("w2", 0), 0, "S")
+                prep_x(("w2", 0), 1, "S")
+                prep_x(("h", 1), 0, "S")
+                prep_x(("h", 1), 1, "S")
+            if i >= 4 and e == 1 and c + 1 < NCHUNK:
+                prep_x(("h", c + 1), 0, "S")
+                prep_x(("h", c + 1), 1, "S")
+            if i < NSTEP and i not in S_REGROUP:
+                regroup(i)
+            pend = due(i)
+            if i == 0:
+                q_w1(2)
+                nc.vector.tensor_scalar(out=gq[:], in0=g_sig[:], scalar1=0.25, scalar2=None, op0=ALU.mult)
+                nc.vector.tensor_copy(out=b2f[:].rearrange("p e a -> p (e a)"), in_=b2_bf[:])
+            if i == 1:
+                q_w1(3)
+            if i == 2:
+                prep_q(("w2", 0), w2_codes[:], w2_scales[:])
+            if len(pend) > 0:
+                y_exit(pend[0])
+            if i < NSTEP:
+                quant1(i)
+            if i == 2:
+                q_h(1)
+            if i >= 4 and e == 1 and c + 1 < NCHUNK:
+                q_h(c + 1)
+            for n, j in enumerate(pend):
+                if n > 0:
+                    y_exit(j)
+                if j % NEXP == NEXP - 1:
+                    store_y(j // NEXP)
+                gate_acc(j)
+                if j % NEXP == NEXP - 1:
+                    store_q(j // NEXP)

@@ -1,8 +1,6 @@
 from contextlib import ExitStack
 
-import concourse.bass as bass
 import concourse.mybir as mybir
-import concourse.tile as tile
 from concourse.masks import make_identity
 
 F32 = mybir.dt.float32
@@ -21,17 +19,37 @@ NACT = 128
 R = M // P
 SUB = 4
 NCHUNK = R // SUB
-NSTEP = NCHUNK * NEXP
 
 FLOPS = 2 * M * H * H * NEXP + 2 * M * H * NACT * NEXP
 
 PINNED = True
-V_EXITS = ((0, 2), (0, 3), (1, 2), (1, 3), (2, 2), (2, 3))
-S_REGROUP = ()
+V_EXITS = ((2, 3), (3, 3))
+S_COLS = 80
+EARLY = 0
+HEAD_SPLIT = True
+TAIL_SPLIT = 1
+
+
+def make_steps():
+    steps = []
+    for c in range(NCHUNK):
+        for e in range(NEXP):
+            if (c == 0 and e == 0 and HEAD_SPLIT) or (c == NCHUNK - 1 and e >= NEXP - TAIL_SPLIT):
+                steps.append((c, 0, 2, e))
+                steps.append((c, 2, 2, e))
+            else:
+                steps.append((c, 0, 4, e))
+    return steps
 
 
 def tile_mspagent_pb_t_kernel(tc, h, gate_logit, e_w1, e_b1, e_w2, e_b2, out_0, out_1):
     nc = tc.nc
+    steps = make_steps()
+    nstep = len(steps)
+    first_step = {}
+    for i in range(nstep):
+        if steps[i][0] not in first_step:
+            first_step[steps[i][0]] = i
     with ExitStack() as ctx:
         const = ctx.enter_context(tc.tile_pool(name="const", bufs=1))
         work = ctx.enter_context(tc.tile_pool(name="work", bufs=2))
@@ -56,30 +74,34 @@ def tile_mspagent_pb_t_kernel(tc, h, gate_logit, e_w1, e_b1, e_w2, e_b2, out_0, 
         h_scales = const.tile([P, NCHUNK, 512], U8, name="h_scales", align_bytes=64)
         w1_codes = const.tile([P, NEXP, 512], U32, name="w1_codes", align_bytes=64)
         w1_scales = const.tile([P, NEXP, 512], U8, name="w1_scales", align_bytes=64)
-        w2_codes = const.tile([P, 512], U32, name="w2_codes", align_bytes=64)
-        w2_scales = const.tile([P, 512], U8, name="w2_scales", align_bytes=64)
+        w2_codes = const.tile([P, 1, 512], U32, name="w2_codes", align_bytes=64)
+        w2_scales = const.tile([P, 1, 512], U8, name="w2_scales", align_bytes=64)
 
         h_view = h.rearrange("(p r) k -> p (r k)", r=R)
         CH = SUB * H
 
-        def load_h(c):
-            nc.sync.dma_start(out=h_sb[:, CH * c : CH * (c + 1)], in_=h_view[:, CH * c : CH * (c + 1)])
+        def load_h(c, lo, hi):
+            nc.sync.dma_start(out=h_sb[:, CH * c + H * lo : CH * c + H * hi], in_=h_view[:, CH * c + H * lo : CH * c + H * hi])
 
-        def load_w1(e):
-            nc.sync.dma_start(out=w1_sb[:, 4 * H * e : 4 * H * (e + 1)], in_=e_w1[e].rearrange("(p t) k -> p (t k)", t=4))
+        def load_w1(e, lo, hi):
+            nc.sync.dma_start(
+                out=w1_sb[:, CH * e + H * lo : CH * e + H * hi],
+                in_=e_w1[e].rearrange("(p t) k -> p (t k)", t=4)[:, H * lo : H * hi],
+            )
 
         nc.scalar.dma_start(out=g_bf[:], in_=gate_logit.rearrange("(p r) e -> p (r e)", r=R))
         nc.scalar.dma_start(out=b1_bf[:], in_=e_b1.rearrange("e (p t) -> p e t", t=4))
-        load_h(0)
-        load_w1(0)
-        load_w1(1)
-        load_w1(2)
-        load_w1(3)
+        load_h(0, 0, 2)
+        load_w1(0, 0, 2)
+        load_h(0, 2, 4)
+        load_w1(0, 2, 4)
+        load_w1(1, 0, 4)
         nc.sync.dma_start(out=w2_sb[:].rearrange("a (e k) -> a e k", e=NEXP), in_=e_w2.rearrange("e a k -> a e k"))
-        load_h(1)
+        load_w1(2, 0, 4)
+        load_w1(3, 0, 4)
         nc.scalar.dma_start(out=b2_bf[:], in_=e_b2.rearrange("e a -> (e a)").partition_broadcast(P))
-        for c in range(2, NCHUNK):
-            load_h(c)
+        for c in range(1, NCHUNK):
+            load_h(c, 0, 4)
 
         make_identity(nc, ident[:])
         nc.scalar.activation(out=g_sig[:], in_=g_bf[:], func=ACT.Sigmoid)
@@ -89,48 +111,41 @@ def tile_mspagent_pb_t_kernel(tc, h, gate_logit, e_w1, e_b1, e_w2, e_b2, out_0, 
         w1_words = w1_sb[:].bitcast(F32)
         w2_words = w2_sb[:].bitcast(F32).rearrange("a (e p u) -> a e u p", e=NEXP, u=2)
 
-        def src_h(c):
-            return lambda j, u: h_words[:, HW * (SUB * c + j) + P * u : HW * (SUB * c + j) + P * (u + 1)]
+        def source(kind, n, j, u):
+            if kind == "h":
+                return h_words[:, HW * (SUB * n + j) + P * u : HW * (SUB * n + j) + P * (u + 1)]
+            if kind == "w1":
+                return w1_words[:, HW * (4 * n + j) + P * u : HW * (4 * n + j) + P * (u + 1)]
+            return w2_words[:, j, u, :]
 
-        def src_w1(e):
-            return lambda j, u: w1_words[:, HW * (4 * e + j) + P * u : HW * (4 * e + j) + P * (u + 1)]
-
-        def src_w2():
-            return lambda j, u: w2_words[:, j, u, :]
-
+        target = {"h": (h_codes, h_scales), "w1": (w1_codes, w1_scales), "w2": (w2_codes, w2_scales)}
         banks = {}
         grouped = {}
 
-        def prep_t(key, src, pool):
-            for b in range(2):
-                tr = pool.tile([P, 2, 2, P], F32, name="tr", tag="bank")
-                for j in range(2):
-                    for u in range(2):
-                        nc.tensor.transpose(tr[:, j, u, :], src(2 * b + j, u), ident[:])
-                banks[(key, b)] = tr
+        def prep_t(kind, n, b, pool):
+            tr = pool.tile([P, 2, 2, P], F32, name="tr", tag="bank")
+            for j in range(2):
+                for u in range(2):
+                    nc.tensor.transpose(tr[:, j, u, :], source(kind, n, 2 * b + j, u), ident[:])
+            banks[(kind, n, b)] = tr
 
-        def prep_x(key, b, eng):
-            if b == 0:
-                grouped[key] = work.tile([P, 4 * P * 4], BF16, name="gp", tag="gp", bufs=3, align_bytes=64)
-            dst = grouped[key][:].bitcast(F32)[:, 512 * b : 512 * (b + 1)].rearrange("p (j c u) -> p j c u", j=2, u=2)
-            src = banks[(key, b)][:].rearrange("p j u c -> p j c u")
+        def prep_x(kind, n, b, eng):
+            if (kind, n) not in grouped:
+                grouped[(kind, n)] = work.tile([P, 4 * P * 4], BF16, name="gp", tag="gp", bufs=4, align_bytes=64)
+            dst = grouped[(kind, n)][:].bitcast(F32)[:, 512 * b : 512 * (b + 1)].rearrange("p (j c u) -> p j c u", j=2, u=2)
+            src = banks[(kind, n, b)][:].rearrange("p j u c -> p j c u")
             if eng == "S":
                 nc.scalar.copy(out=dst, in_=src)
             else:
                 nc.vector.tensor_copy(out=dst, in_=src)
 
-        def prep_q(key, codes, scales):
+        def prep_q(kind, n, lo, hi):
+            codes, scales = target[kind]
             nc.vector.quantize_mx(
-                out=codes.bitcast(FP8X4),
-                scales=scales,
-                in_=grouped[key][:],
+                out=codes[:, n, 256 * lo : 256 * hi].bitcast(FP8X4),
+                scales=scales[:, n, 256 * lo : 256 * hi],
+                in_=grouped[(kind, n)][:, 1024 * lo : 1024 * hi],
             )
-
-        def q_h(c):
-            prep_q(("h", c), h_codes[:, c, :], h_scales[:, c, :])
-
-        def q_w1(e):
-            prep_q(("w1", e), w1_codes[:, e, :], w1_scales[:, e, :])
 
         acc = {}
         planar = {}
@@ -141,79 +156,90 @@ def tile_mspagent_pb_t_kernel(tc, h, gate_logit, e_w1, e_b1, e_w2, e_b2, out_0, 
         qtile = {}
 
         def stage1(i, t):
-            c, e = divmod(i, NEXP)
+            c, s0, ns, e = steps[i]
             a = ps_s1.tile([P, 512], F32, name="acc", tag="bank")
             nc.tensor.matmul_mx(
-                out=a[:],
+                out=a[:, : P * ns],
                 lhsT=w1_codes[:, e, P * t : P * (t + 1)].bitcast(FP8X4),
                 lhsT_scale=w1_scales[:, e, P * t : P * (t + 1)],
-                rhs=h_codes[:, c, :].bitcast(FP8X4),
-                rhs_scale=h_scales[:, c, :],
+                rhs=h_codes[:, c, P * s0 : P * (s0 + ns)].bitcast(FP8X4),
+                rhs_scale=h_scales[:, c, P * s0 : P * (s0 + ns)],
                 start=True,
                 stop=True,
             )
             acc[(i, t)] = a
 
         def exit1(i, t):
-            e = i % NEXP
+            c, s0, ns, e = steps[i]
+            w = P * ns
             if t == 0:
                 planar[i] = work.tile([P, 4, 512], BF16, name="planar", tag="planar", bufs=3)
             bias = b1f[:, 4 * e + t : 4 * e + t + 1]
             if (i, t) in V_EXITS:
                 nc.vector.tensor_scalar(
-                    out=planar[i][:, t, :], in0=acc[(i, t)][:], scalar1=bias, scalar2=0.0, op0=ALU.add, op1=ALU.max
+                    out=planar[i][:, t, :w], in0=acc[(i, t)][:, :w], scalar1=bias, scalar2=0.0, op0=ALU.add, op1=ALU.max
                 )
             else:
-                nc.scalar.activation(out=planar[i][:, t, :], in_=acc[(i, t)][:], func=ACT.Relu, bias=bias, scale=1.0)
+                nc.scalar.activation(out=planar[i][:, t, :w], in_=acc[(i, t)][:, :w], func=ACT.Relu, bias=bias, scale=1.0)
 
-        def regroup(i):
-            g = work.tile([P, 512, 4], BF16, name="inter", tag="inter", bufs=2, align_bytes=64)
-            dst = g[:].rearrange("p (c i) t -> p c t i", i=4)
-            src = planar[i][:].rearrange("p t (c i) -> p c t i", i=4)
-            if i in S_REGROUP:
+        def regroup(i, eng):
+            c, s0, ns, e = steps[i]
+            w = P * ns
+            cut = w - ((S_COLS * ns) // SUB if i >= EARLY else 0)
+            if i not in inter:
+                inter[i] = work.tile([P, 512, 4], BF16, name="inter", tag="inter", bufs=3, align_bytes=64)
+            lo, hi = (cut, w) if eng == "S" else (0, cut)
+            if lo == hi:
+                return
+            dst = inter[i][:, lo:hi, :].rearrange("p (c i) t -> p c t i", i=4)
+            src = planar[i][:, :, lo:hi].rearrange("p t (c i) -> p c t i", i=4)
+            if eng == "S":
                 nc.scalar.copy(out=dst, in_=src)
             else:
                 nc.vector.tensor_copy(out=dst, in_=src)
-            inter[i] = g
 
         def quant1(i):
+            c, s0, ns, e = steps[i]
+            w = P * ns
             cd = work.tile([P, 512], U32, name="cd1", tag="cd1", bufs=4, align_bytes=64)
             sc = work.tile([P, 512], U8, name="sc1", tag="sc1", bufs=4, align_bytes=64)
-            nc.vector.quantize_mx(out=cd[:].bitcast(FP8X4), scales=sc[:], in_=inter[i][:].rearrange("p c t -> p (c t)"))
+            nc.vector.quantize_mx(
+                out=cd[:, :w].bitcast(FP8X4), scales=sc[:, :w], in_=inter[i][:, :w, :].rearrange("p c t -> p (c t)")
+            )
             codes1[i] = (cd, sc)
 
         def stage2(i):
-            e = i % NEXP
+            c, s0, ns, e = steps[i]
             cd, sc = codes1[i]
             a2 = ps_s2.tile([P, SUB, NACT], F32, name="acc2", tag="bank")
-            for s in range(SUB):
+            for s in range(ns):
                 nc.tensor.matmul_mx(
                     out=a2[:, s, :],
                     lhsT=cd[:, P * s : P * (s + 1)].bitcast(FP8X4),
                     lhsT_scale=sc[:, P * s : P * (s + 1)],
-                    rhs=w2_codes[:, NACT * e : NACT * (e + 1)].bitcast(FP8X4),
-                    rhs_scale=w2_scales[:, NACT * e : NACT * (e + 1)],
+                    rhs=w2_codes[:, 0, NACT * e : NACT * (e + 1)].bitcast(FP8X4),
+                    rhs_scale=w2_scales[:, 0, NACT * e : NACT * (e + 1)],
                     start=True,
                     stop=True,
                 )
             acc2[i] = a2
 
         def y_exit(i):
-            c, e = divmod(i, NEXP)
-            if e == 0:
+            c, s0, ns, e = steps[i]
+            if c not in ytile:
                 ytile[c] = work.tile([P, SUB, NEXP, NACT], F32, name="y", tag="y", bufs=3)
             nc.vector.tensor_tensor(
-                out=ytile[c][:, :, e, :],
-                in0=acc2[i][:],
-                in1=b2f[:, e, :].unsqueeze(1).to_broadcast([P, SUB, NACT]),
+                out=ytile[c][:, s0 : s0 + ns, e, :],
+                in0=acc2[i][:, :ns, :],
+                in1=b2f[:, e, :].unsqueeze(1).to_broadcast([P, ns, NACT]),
                 op=ALU.add,
             )
 
         def gate_acc(i):
-            c, e = divmod(i, NEXP)
-            if e == 0:
+            c, s0, ns, e = steps[i]
+            if c not in qtile:
                 qtile[c] = work.tile([P, SUB, NACT], F32, name="q", tag="q", bufs=3)
-            for s in range(SUB):
+            for s in range(s0, s0 + ns):
                 col = (SUB * c + s) * NEXP + e
                 if e == 0:
                     nc.vector.tensor_scalar(
@@ -232,94 +258,115 @@ def tile_mspagent_pb_t_kernel(tc, h, gate_logit, e_w1, e_b1, e_w2, e_b2, out_0, 
         out1_view = out_1.rearrange("(p r) e a -> p r (e a)", r=R)
         out0_view = out_0.rearrange("(p r) a -> p r a", r=R)
 
-        def store_y(c):
-            nc.sync.dma_start(out=out1_view[:, SUB * c : SUB * (c + 1), :], in_=ytile[c][:].rearrange("p s e a -> p s (e a)"))
+        def store_y(c, s0, ns):
+            nc.sync.dma_start(
+                out=out1_view[:, SUB * c + s0 : SUB * c + s0 + ns, :],
+                in_=ytile[c][:, s0 : s0 + ns, :, :].rearrange("p s e a -> p s (e a)"),
+            )
 
-        def store_q(c):
-            nc.sync.dma_start(out=out0_view[:, SUB * c : SUB * (c + 1), :], in_=qtile[c][:])
+        def store_q(c, s0, ns):
+            nc.sync.dma_start(out=out0_view[:, SUB * c + s0 : SUB * c + s0 + ns, :], in_=qtile[c][:, s0 : s0 + ns, :])
 
-        prep_t(("h", 0), src_h(0), ps_tr)
-        prep_x(("h", 0), 0, "S")
-        prep_x(("h", 0), 1, "V")
-        prep_t(("w1", 0), src_w1(0), ps_s2)
-        q_h(0)
-        prep_x(("w1", 0), 0, "S")
-        prep_x(("w1", 0), 1, "V")
-        prep_t(("w1", 1), src_w1(1), ps_tr)
+        prep_t("h", 0, 0, ps_tr)
+        prep_x("h", 0, 0, "S")
+        prep_t("w1", 0, 0, ps_s2)
+        prep_x("w1", 0, 0, "V")
+        prep_q("h", 0, 0, 1)
+        prep_t("h", 0, 1, ps_tr)
+        prep_x("h", 0, 1, "S")
+        prep_q("w1", 0, 0, 1)
+        prep_t("w1", 0, 1, ps_s2)
         nc.vector.tensor_copy(out=b1f[:], in_=b1_bf[:].rearrange("p e t -> p (e t)"))
-        q_w1(0)
-        prep_x(("w1", 1), 0, "S")
-        prep_x(("w1", 1), 1, "S")
-        for t in range(4):
-            stage1(0, t)
-        prep_t(("w1", 2), src_w1(2), ps_s2)
-        q_w1(1)
+        prep_x("w1", 0, 1, "V")
+        stage1(0, 0)
+        stage1(0, 1)
+        prep_t("w1", 1, 0, ps_tr)
+        prep_t("w1", 1, 1, ps_tr)
+        prep_q("w1", 0, 1, 2)
+        prep_q("h", 0, 1, 2)
+        stage1(0, 2)
+        stage1(0, 3)
+        prep_x("w1", 1, 0, "V")
+        prep_x("w1", 1, 1, "V")
+        nc.vector.tensor_scalar(out=gq[:], in0=g_sig[:], scalar1=0.25, scalar2=None, op0=ALU.mult)
+        prep_q("w1", 1, 0, 2)
+
+        extra = {}
+
+        def add(i, place, item):
+            extra[(i, place)] = extra.get((i, place), []) + [item]
+
+        add(0, "pe", ("T", "w2", 0, 0, ps_s2))
+        add(0, "pe", ("T", "w2", 0, 1, ps_s2))
+        add(0, "pe", ("T", "w1", 2, 0, ps_tr))
+        add(0, "pe", ("T", "w1", 2, 1, ps_tr))
+        add(1, "s", ("X", "w2", 0, 0, "S"))
+        add(1, "s", ("X", "w2", 0, 1, "S"))
+        add(1, "s", ("X", "w1", 2, 0, "S"))
+        add(1, "s", ("X", "w1", 2, 1, "S"))
+        add(1, "v2", ("Q", "w2", 0, 0, 2))
+        add(1, "v2", ("Q", "w1", 2, 0, 2))
+        add(1, "pe", ("T", "w1", 3, 0, ps_tr))
+        add(1, "pe", ("T", "w1", 3, 1, ps_tr))
+        add(2, "s", ("X", "w1", 3, 0, "S"))
+        add(2, "s", ("X", "w1", 3, 1, "S"))
+        add(2, "v2", ("Q", "w1", 3, 0, 2))
+        for c in range(1, NCHUNK):
+            f = first_step[c]
+            add(f - 4, "pe", ("T", "h", c, 0, ps_tr))
+            add(f - 4, "pe", ("T", "h", c, 1, ps_tr))
+            add(f - 3, "s", ("X", "h", c, 0, "S"))
+            add(f - 3, "s", ("X", "h", c, 1, "S"))
+            add(f - 3, "v2", ("Q", "h", c, 0, 2))
+
+        def run(i, place):
+            for op, kind, n, x, y in extra.get((i, place), []):
+                if op == "T":
+                    prep_t(kind, n, x, y)
+                elif op == "X":
+                    prep_x(kind, n, x, y)
+                else:
+                    prep_q(kind, n, x, y)
+
+        LAG0 = 2
 
         def due(i):
-            if i < 3:
+            if i < LAG0:
                 return []
-            if i == 3:
-                return [0, 1]
-            if i == 4:
-                return [2, 3]
+            if i == LAG0:
+                return list(range(0, LAG0))
             return [i - 1]
 
-        for i in range(NSTEP + 1):
-            c, e = divmod(i, NEXP)
-            if i < NSTEP:
+        for i in range(nstep + 1):
+            if i < nstep:
                 for t in range(4):
                     exit1(i, t)
-                    if i + 1 < NSTEP:
+                    run(i, t)
+                    if i + 1 < nstep:
                         stage1(i + 1, t)
-                if i in S_REGROUP:
-                    regroup(i)
-            for j in due(i):
-                stage2(j)
-            if i == 0:
-                prep_t(("w1", 3), src_w1(3), ps_tr)
-            if i == 1:
-                prep_t(("w2", 0), src_w2(), ps_s2)
-                prep_t(("h", 1), src_h(1), ps_tr)
-            if i >= 4 and e == 0 and c + 1 < NCHUNK:
-                prep_t(("h", c + 1), src_h(c + 1), ps_tr)
-            if i == 0:
-                prep_x(("w1", 2), 0, "S")
-                prep_x(("w1", 2), 1, "S")
-            if i == 1:
-                prep_x(("w1", 3), 0, "S")
-                prep_x(("w1", 3), 1, "S")
-            if i == 2:
-                prep_x(("w2", 0), 0, "S")
-                prep_x(("w2", 0), 1, "S")
-                prep_x(("h", 1), 0, "S")
-                prep_x(("h", 1), 1, "S")
-            if i >= 4 and e == 1 and c + 1 < NCHUNK:
-                prep_x(("h", c + 1), 0, "S")
-                prep_x(("h", c + 1), 1, "S")
-            if i < NSTEP and i not in S_REGROUP:
-                regroup(i)
+                regroup(i, "S")
             pend = due(i)
-            if i == 0:
-                q_w1(2)
-                nc.vector.tensor_scalar(out=gq[:], in0=g_sig[:], scalar1=0.25, scalar2=None, op0=ALU.mult)
-                nc.vector.tensor_copy(out=b2f[:].rearrange("p e a -> p (e a)"), in_=b2_bf[:])
+            for j in pend:
+                stage2(j)
+            run(i, "pe")
+            run(i, "s")
+            run(i, "v0")
+            if i < nstep:
+                regroup(i, "V")
+            run(i, "v1")
             if i == 1:
-                q_w1(3)
-            if i == 2:
-                prep_q(("w2", 0), w2_codes[:], w2_scales[:])
+                nc.vector.tensor_copy(out=b2f[:].rearrange("p e a -> p (e a)"), in_=b2_bf[:])
             if len(pend) > 0:
                 y_exit(pend[0])
-            if i < NSTEP:
+            if i < nstep:
                 quant1(i)
-            if i == 2:
-                q_h(1)
-            if i >= 4 and e == 1 and c + 1 < NCHUNK:
-                q_h(c + 1)
+            run(i, "v2")
             for n, j in enumerate(pend):
+                c, s0, ns, e = steps[j]
                 if n > 0:
                     y_exit(j)
-                if j % NEXP == NEXP - 1:
-                    store_y(j // NEXP)
+                if e == NEXP - 1:
+                    store_y(c, s0, ns)
                 gate_acc(j)
-                if j % NEXP == NEXP - 1:
-                    store_q(j // NEXP)
+                if e == NEXP - 1:
+                    store_q(c, s0, ns)

@@ -12,6 +12,7 @@ ACT = mybir.ActivationFunctionType
 ALU = mybir.AluOpType
 
 P = 128
+PACK = 4
 M = 4096
 H = 512
 NEXP = 4
@@ -19,78 +20,68 @@ NACT = 128
 R = M // P
 SUB = 4
 NCHUNK = R // SUB
+CHUNK = SUB * P
+WORDS = H // 2
 
 FLOPS = 2 * M * H * H * NEXP + 2 * M * H * NACT * NEXP
 
-PINNED = True
-V_EXITS = ((2, 3), (3, 3))
-S_COLS = 80
-EARLY = 0
-HEAD_SPLIT = True
-TAIL_SPLIT = 1
 
-
-def make_steps():
+def step_list():
     steps = []
     for c in range(NCHUNK):
         for e in range(NEXP):
-            if (c == 0 and e == 0 and HEAD_SPLIT) or (c == NCHUNK - 1 and e >= NEXP - TAIL_SPLIT):
-                steps.append((c, 0, 2, e))
-                steps.append((c, 2, 2, e))
+            if (c == 0 and e == 0) or (c == NCHUNK - 1 and e == NEXP - 1):
+                steps.append((c, 0, SUB // 2, e))
+                steps.append((c, SUB // 2, SUB // 2, e))
             else:
-                steps.append((c, 0, 4, e))
+                steps.append((c, 0, SUB, e))
     return steps
 
 
 def tile_mspagent_pb_t_kernel(tc, h, gate_logit, e_w1, e_b1, e_w2, e_b2, out_0, out_1):
     nc = tc.nc
-    steps = make_steps()
+    steps = step_list()
     nstep = len(steps)
-    first_step = {}
-    for i in range(nstep):
-        if steps[i][0] not in first_step:
-            first_step[steps[i][0]] = i
     with ExitStack() as ctx:
         const = ctx.enter_context(tc.tile_pool(name="const", bufs=1))
         work = ctx.enter_context(tc.tile_pool(name="work", bufs=2))
         ps_s1 = ctx.enter_context(tc.psum_pool(name="ps_s1", bufs=4))
         ps_s2 = ctx.enter_context(tc.psum_pool(name="ps_s2", bufs=2))
         ps_tr = ctx.enter_context(tc.psum_pool(name="ps_tr", bufs=2))
-        if PINNED:
-            ctx.enter_context(tc.manual_schedule())
+        ctx.enter_context(tc.manual_schedule())
 
         h_sb = const.tile([P, R * H], BF16, name="h_sb")
-        w1_sb = const.tile([P, NEXP * 4 * H], BF16, name="w1_sb")
+        w1_sb = const.tile([P, NEXP * PACK * H], BF16, name="w1_sb")
         w2_sb = const.tile([P, NEXP * H], BF16, name="w2_sb")
-        b1_bf = const.tile([P, NEXP, 4], BF16, name="b1_bf")
-        b1f = const.tile([P, NEXP * 4], F32, name="b1f")
+        b1_bf = const.tile([P, NEXP, PACK], BF16, name="b1_bf")
+        b1 = const.tile([P, NEXP * PACK], F32, name="b1")
         b2_bf = const.tile([P, NEXP * NACT], BF16, name="b2_bf")
-        b2f = const.tile([P, NEXP, NACT], F32, name="b2f")
-        g_bf = const.tile([P, R * NEXP], BF16, name="g_bf")
-        g_sig = const.tile([P, R * NEXP], F32, name="g_sig")
-        gq = const.tile([P, R * NEXP], F32, name="gq")
+        b2 = const.tile([P, NEXP, NACT], F32, name="b2")
+        gate_bf = const.tile([P, R * NEXP], BF16, name="gate_bf")
+        gate_sig = const.tile([P, R * NEXP], F32, name="gate_sig")
+        gate = const.tile([P, R * NEXP], F32, name="gate")
         ident = const.tile([P, P], F32, name="ident")
-        h_codes = const.tile([P, NCHUNK, 512], U32, name="h_codes", align_bytes=64)
-        h_scales = const.tile([P, NCHUNK, 512], U8, name="h_scales", align_bytes=64)
-        w1_codes = const.tile([P, NEXP, 512], U32, name="w1_codes", align_bytes=64)
-        w1_scales = const.tile([P, NEXP, 512], U8, name="w1_scales", align_bytes=64)
-        w2_codes = const.tile([P, 1, 512], U32, name="w2_codes", align_bytes=64)
-        w2_scales = const.tile([P, 1, 512], U8, name="w2_scales", align_bytes=64)
+        h_codes = const.tile([P, NCHUNK, CHUNK], U32, name="h_codes", align_bytes=64)
+        h_scales = const.tile([P, NCHUNK, CHUNK], U8, name="h_scales", align_bytes=64)
+        w1_codes = const.tile([P, NEXP, PACK * P], U32, name="w1_codes", align_bytes=64)
+        w1_scales = const.tile([P, NEXP, PACK * P], U8, name="w1_scales", align_bytes=64)
+        w2_codes = const.tile([P, 1, NEXP * NACT], U32, name="w2_codes", align_bytes=64)
+        w2_scales = const.tile([P, 1, NEXP * NACT], U8, name="w2_scales", align_bytes=64)
 
-        h_view = h.rearrange("(p r) k -> p (r k)", r=R)
-        CH = SUB * H
+        h_rows = h.rearrange("(p r) k -> p (r k)", r=R)
 
         def load_h(c, lo, hi):
-            nc.sync.dma_start(out=h_sb[:, CH * c + H * lo : CH * c + H * hi], in_=h_view[:, CH * c + H * lo : CH * c + H * hi])
+            cols = slice((SUB * c + lo) * H, (SUB * c + hi) * H)
+            nc.sync.dma_start(out=h_sb[:, cols], in_=h_rows[:, cols])
 
         def load_w1(e, lo, hi):
             nc.sync.dma_start(
-                out=w1_sb[:, CH * e + H * lo : CH * e + H * hi],
-                in_=e_w1[e].rearrange("(p t) k -> p (t k)", t=4)[:, H * lo : H * hi],
+                out=w1_sb[:, (PACK * e + lo) * H : (PACK * e + hi) * H],
+                in_=e_w1[e].rearrange("(p t) k -> p (t k)", t=PACK)[:, lo * H : hi * H],
             )
 
-        nc.scalar.dma_start(out=g_bf[:], in_=gate_logit.rearrange("(p r) e -> p (r e)", r=R))
-        nc.scalar.dma_start(out=b1_bf[:], in_=e_b1.rearrange("e (p t) -> p e t", t=4))
+        nc.scalar.dma_start(out=gate_bf[:], in_=gate_logit.rearrange("(p r) e -> p (r e)", r=R))
+        nc.scalar.dma_start(out=b1_bf[:], in_=e_b1.rearrange("e (p t) -> p e t", t=PACK))
         load_h(0, 0, 2)
         load_w1(0, 0, 2)
         load_h(0, 2, 4)
@@ -104,62 +95,64 @@ def tile_mspagent_pb_t_kernel(tc, h, gate_logit, e_w1, e_b1, e_w2, e_b2, out_0, 
             load_h(c, 0, 4)
 
         make_identity(nc, ident[:])
-        nc.scalar.activation(out=g_sig[:], in_=g_bf[:], func=ACT.Sigmoid)
+        nc.scalar.activation(out=gate_sig[:], in_=gate_bf[:], func=ACT.Sigmoid)
 
-        HW = H // 2
         h_words = h_sb[:].bitcast(F32)
         w1_words = w1_sb[:].bitcast(F32)
         w2_words = w2_sb[:].bitcast(F32).rearrange("a (e p u) -> a e u p", e=NEXP, u=2)
 
-        def source(kind, n, j, u):
+        def block_words(kind, n, j, u):
             if kind == "h":
-                return h_words[:, HW * (SUB * n + j) + P * u : HW * (SUB * n + j) + P * (u + 1)]
+                first = (SUB * n + j) * WORDS + P * u
+                return h_words[:, first : first + P]
             if kind == "w1":
-                return w1_words[:, HW * (4 * n + j) + P * u : HW * (4 * n + j) + P * (u + 1)]
+                first = (PACK * n + j) * WORDS + P * u
+                return w1_words[:, first : first + P]
             return w2_words[:, j, u, :]
 
-        target = {"h": (h_codes, h_scales), "w1": (w1_codes, w1_scales), "w2": (w2_codes, w2_scales)}
-        banks = {}
-        grouped = {}
+        quantised = {"h": (h_codes, h_scales), "w1": (w1_codes, w1_scales), "w2": (w2_codes, w2_scales)}
+        bank_of = {}
+        grouped_of = {}
 
-        def prep_t(kind, n, b, pool):
-            tr = pool.tile([P, 2, 2, P], F32, name="tr", tag="bank")
+        def transpose_half(kind, n, half, pool):
+            bank = pool.tile([P, 2, 2, P], F32, name="tr", tag="bank")
             for j in range(2):
                 for u in range(2):
-                    nc.tensor.transpose(tr[:, j, u, :], source(kind, n, 2 * b + j, u), ident[:])
-            banks[(kind, n, b)] = tr
+                    nc.tensor.transpose(bank[:, j, u, :], block_words(kind, n, 2 * half + j, u), ident[:])
+            bank_of[(kind, n, half)] = bank
 
-        def prep_x(kind, n, b, eng):
-            if (kind, n) not in grouped:
-                grouped[(kind, n)] = work.tile([P, 4 * P * 4], BF16, name="gp", tag="gp", bufs=4, align_bytes=64)
-            dst = grouped[(kind, n)][:].bitcast(F32)[:, 512 * b : 512 * (b + 1)].rearrange("p (j c u) -> p j c u", j=2, u=2)
-            src = banks[(kind, n, b)][:].rearrange("p j u c -> p j c u")
-            if eng == "S":
+        def copy_half(kind, n, half, engine):
+            if (kind, n) not in grouped_of:
+                grouped_of[(kind, n)] = work.tile([P, PACK * P * PACK], BF16, name="grouped", tag="grouped", bufs=4, align_bytes=64)
+            dst = grouped_of[(kind, n)][:].bitcast(F32)[:, 512 * half : 512 * (half + 1)]
+            dst = dst.rearrange("p (j c u) -> p j c u", j=2, u=2)
+            src = bank_of[(kind, n, half)][:].rearrange("p j u c -> p j c u")
+            if engine == "scalar":
                 nc.scalar.copy(out=dst, in_=src)
             else:
                 nc.vector.tensor_copy(out=dst, in_=src)
 
-        def prep_q(kind, n, lo, hi):
-            codes, scales = target[kind]
+        def quantise_halves(kind, n, lo, hi):
+            codes, scales = quantised[kind]
             nc.vector.quantize_mx(
                 out=codes[:, n, 256 * lo : 256 * hi].bitcast(FP8X4),
                 scales=scales[:, n, 256 * lo : 256 * hi],
-                in_=grouped[(kind, n)][:, 1024 * lo : 1024 * hi],
+                in_=grouped_of[(kind, n)][:, 1024 * lo : 1024 * hi],
             )
 
-        acc = {}
-        planar = {}
-        inter = {}
-        codes1 = {}
-        acc2 = {}
-        ytile = {}
-        qtile = {}
+        acc1_of = {}
+        planes_of = {}
+        packed_of = {}
+        h1_of = {}
+        acc2_of = {}
+        y_of = {}
+        q_of = {}
 
         def stage1(i, t):
             c, s0, ns, e = steps[i]
-            a = ps_s1.tile([P, 512], F32, name="acc", tag="bank")
+            acc1 = ps_s1.tile([P, CHUNK], F32, name="acc1", tag="bank")
             nc.tensor.matmul_mx(
-                out=a[:, : P * ns],
+                out=acc1[:, : P * ns],
                 lhsT=w1_codes[:, e, P * t : P * (t + 1)].bitcast(FP8X4),
                 lhsT_scale=w1_scales[:, e, P * t : P * (t + 1)],
                 rhs=h_codes[:, c, P * s0 : P * (s0 + ns)].bitcast(FP8X4),
@@ -167,206 +160,156 @@ def tile_mspagent_pb_t_kernel(tc, h, gate_logit, e_w1, e_b1, e_w2, e_b2, out_0, 
                 start=True,
                 stop=True,
             )
-            acc[(i, t)] = a
+            acc1_of[(i, t)] = acc1
 
         def exit1(i, t):
             c, s0, ns, e = steps[i]
-            w = P * ns
             if t == 0:
-                planar[i] = work.tile([P, 4, 512], BF16, name="planar", tag="planar", bufs=3)
-            bias = b1f[:, 4 * e + t : 4 * e + t + 1]
-            if (i, t) in V_EXITS:
-                nc.vector.tensor_scalar(
-                    out=planar[i][:, t, :w], in0=acc[(i, t)][:, :w], scalar1=bias, scalar2=0.0, op0=ALU.add, op1=ALU.max
-                )
-            else:
-                nc.scalar.activation(out=planar[i][:, t, :w], in_=acc[(i, t)][:, :w], func=ACT.Relu, bias=bias, scale=1.0)
+                planes_of[i] = work.tile([P, PACK, CHUNK], BF16, name="planes", tag="planes", bufs=4)
+            nc.scalar.activation(
+                out=planes_of[i][:, t, : P * ns],
+                in_=acc1_of[(i, t)][:, : P * ns],
+                func=ACT.Relu,
+                bias=b1[:, PACK * e + t : PACK * e + t + 1],
+                scale=1.0,
+            )
 
-        def regroup(i, eng):
+        def by_scalar(i):
+            return (i > 0 and i % 12 == 0) or i >= nstep - 2
+
+        def regroup(i):
             c, s0, ns, e = steps[i]
-            w = P * ns
-            cut = w - ((S_COLS * ns) // SUB if i >= EARLY else 0)
-            if i not in inter:
-                inter[i] = work.tile([P, 512, 4], BF16, name="inter", tag="inter", bufs=3, align_bytes=64)
-            lo, hi = (cut, w) if eng == "S" else (0, cut)
-            if lo == hi:
-                return
-            dst = inter[i][:, lo:hi, :].rearrange("p (c i) t -> p c t i", i=4)
-            src = planar[i][:, :, lo:hi].rearrange("p t (c i) -> p c t i", i=4)
-            if eng == "S":
+            packed_of[i] = work.tile([P, CHUNK, PACK], BF16, name="packed", tag="packed", bufs=3, align_bytes=64)
+            dst = packed_of[i][:, : P * ns, :].rearrange("p (c i) t -> p c t i", i=4)
+            src = planes_of[i][:, :, : P * ns].rearrange("p t (c i) -> p c t i", i=4)
+            if by_scalar(i):
                 nc.scalar.copy(out=dst, in_=src)
             else:
                 nc.vector.tensor_copy(out=dst, in_=src)
 
-        def quant1(i):
+        def quantise_h1(i):
             c, s0, ns, e = steps[i]
-            w = P * ns
-            cd = work.tile([P, 512], U32, name="cd1", tag="cd1", bufs=4, align_bytes=64)
-            sc = work.tile([P, 512], U8, name="sc1", tag="sc1", bufs=4, align_bytes=64)
+            codes = work.tile([P, CHUNK], U32, name="h1_codes", tag="h1_codes", bufs=4, align_bytes=64)
+            scales = work.tile([P, CHUNK], U8, name="h1_scales", tag="h1_scales", bufs=4, align_bytes=64)
             nc.vector.quantize_mx(
-                out=cd[:, :w].bitcast(FP8X4), scales=sc[:, :w], in_=inter[i][:, :w, :].rearrange("p c t -> p (c t)")
+                out=codes[:, : P * ns].bitcast(FP8X4),
+                scales=scales[:, : P * ns],
+                in_=packed_of[i][:, : P * ns, :].rearrange("p c t -> p (c t)"),
             )
-            codes1[i] = (cd, sc)
+            h1_of[i] = (codes, scales)
 
         def stage2(i):
             c, s0, ns, e = steps[i]
-            cd, sc = codes1[i]
-            a2 = ps_s2.tile([P, SUB, NACT], F32, name="acc2", tag="bank")
+            codes, scales = h1_of[i]
+            acc2 = ps_s2.tile([P, SUB, NACT], F32, name="acc2", tag="bank")
             for s in range(ns):
                 nc.tensor.matmul_mx(
-                    out=a2[:, s, :],
-                    lhsT=cd[:, P * s : P * (s + 1)].bitcast(FP8X4),
-                    lhsT_scale=sc[:, P * s : P * (s + 1)],
+                    out=acc2[:, s, :],
+                    lhsT=codes[:, P * s : P * (s + 1)].bitcast(FP8X4),
+                    lhsT_scale=scales[:, P * s : P * (s + 1)],
                     rhs=w2_codes[:, 0, NACT * e : NACT * (e + 1)].bitcast(FP8X4),
                     rhs_scale=w2_scales[:, 0, NACT * e : NACT * (e + 1)],
                     start=True,
                     stop=True,
                 )
-            acc2[i] = a2
+            acc2_of[i] = acc2
 
-        def y_exit(i):
+        def add_b2(i):
             c, s0, ns, e = steps[i]
-            if c not in ytile:
-                ytile[c] = work.tile([P, SUB, NEXP, NACT], F32, name="y", tag="y", bufs=3)
+            if c not in y_of:
+                y_of[c] = work.tile([P, SUB, NEXP, NACT], F32, name="y", tag="y", bufs=3)
             nc.vector.tensor_tensor(
-                out=ytile[c][:, s0 : s0 + ns, e, :],
-                in0=acc2[i][:, :ns, :],
-                in1=b2f[:, e, :].unsqueeze(1).to_broadcast([P, ns, NACT]),
+                out=y_of[c][:, s0 : s0 + ns, e, :],
+                in0=acc2_of[i][:, :ns, :],
+                in1=b2[:, e, :].unsqueeze(1).to_broadcast([P, ns, NACT]),
                 op=ALU.add,
             )
 
-        def gate_acc(i):
+        def add_gated(i):
             c, s0, ns, e = steps[i]
-            if c not in qtile:
-                qtile[c] = work.tile([P, SUB, NACT], F32, name="q", tag="q", bufs=3)
+            if c not in q_of:
+                q_of[c] = work.tile([P, SUB, NACT], F32, name="q", tag="q", bufs=3)
             for s in range(s0, s0 + ns):
-                col = (SUB * c + s) * NEXP + e
+                g = gate[:, (SUB * c + s) * NEXP + e : (SUB * c + s) * NEXP + e + 1]
                 if e == 0:
-                    nc.vector.tensor_scalar(
-                        out=qtile[c][:, s, :], in0=ytile[c][:, s, e, :], scalar1=gq[:, col : col + 1], scalar2=None, op0=ALU.mult
-                    )
+                    nc.vector.tensor_scalar(out=q_of[c][:, s, :], in0=y_of[c][:, s, e, :], scalar1=g, scalar2=None, op0=ALU.mult)
                 else:
                     nc.vector.scalar_tensor_tensor(
-                        out=qtile[c][:, s, :],
-                        in0=ytile[c][:, s, e, :],
-                        scalar=gq[:, col : col + 1],
-                        in1=qtile[c][:, s, :],
-                        op0=ALU.mult,
-                        op1=ALU.add,
+                        out=q_of[c][:, s, :], in0=y_of[c][:, s, e, :], scalar=g, in1=q_of[c][:, s, :], op0=ALU.mult, op1=ALU.add
                     )
 
-        out1_view = out_1.rearrange("(p r) e a -> p r (e a)", r=R)
-        out0_view = out_0.rearrange("(p r) a -> p r a", r=R)
+        out1_rows = out_1.rearrange("(p r) e a -> p r (e a)", r=R)
+        out0_rows = out_0.rearrange("(p r) a -> p r a", r=R)
 
         def store_y(c, s0, ns):
             nc.sync.dma_start(
-                out=out1_view[:, SUB * c + s0 : SUB * c + s0 + ns, :],
-                in_=ytile[c][:, s0 : s0 + ns, :, :].rearrange("p s e a -> p s (e a)"),
+                out=out1_rows[:, SUB * c + s0 : SUB * c + s0 + ns, :],
+                in_=y_of[c][:, s0 : s0 + ns, :, :].rearrange("p s e a -> p s (e a)"),
             )
 
         def store_q(c, s0, ns):
-            nc.sync.dma_start(out=out0_view[:, SUB * c + s0 : SUB * c + s0 + ns, :], in_=qtile[c][:, s0 : s0 + ns, :])
+            nc.sync.dma_start(out=out0_rows[:, SUB * c + s0 : SUB * c + s0 + ns, :], in_=q_of[c][:, s0 : s0 + ns, :])
 
-        prep_t("h", 0, 0, ps_tr)
-        prep_x("h", 0, 0, "S")
-        prep_t("w1", 0, 0, ps_s2)
-        prep_x("w1", 0, 0, "V")
-        prep_q("h", 0, 0, 1)
-        prep_t("h", 0, 1, ps_tr)
-        prep_x("h", 0, 1, "S")
-        prep_q("w1", 0, 0, 1)
-        prep_t("w1", 0, 1, ps_s2)
-        nc.vector.tensor_copy(out=b1f[:], in_=b1_bf[:].rearrange("p e t -> p (e t)"))
-        prep_x("w1", 0, 1, "V")
+        transpose_half("h", 0, 0, ps_tr)
+        copy_half("h", 0, 0, "scalar")
+        transpose_half("w1", 0, 0, ps_s2)
+        copy_half("w1", 0, 0, "vector")
+        quantise_halves("h", 0, 0, 1)
+        transpose_half("h", 0, 1, ps_tr)
+        copy_half("h", 0, 1, "scalar")
+        quantise_halves("w1", 0, 0, 1)
+        transpose_half("w1", 0, 1, ps_s2)
+        nc.vector.tensor_copy(out=b1[:], in_=b1_bf[:].rearrange("p e t -> p (e t)"))
+        copy_half("w1", 0, 1, "vector")
         stage1(0, 0)
         stage1(0, 1)
-        prep_t("w1", 1, 0, ps_tr)
-        prep_t("w1", 1, 1, ps_tr)
-        prep_q("w1", 0, 1, 2)
-        prep_q("h", 0, 1, 2)
+        transpose_half("w1", 1, 0, ps_tr)
+        transpose_half("w1", 1, 1, ps_tr)
+        quantise_halves("w1", 0, 1, 2)
+        quantise_halves("h", 0, 1, 2)
         stage1(0, 2)
         stage1(0, 3)
-        prep_x("w1", 1, 0, "V")
-        prep_x("w1", 1, 1, "V")
-        nc.vector.tensor_scalar(out=gq[:], in0=g_sig[:], scalar1=0.25, scalar2=None, op0=ALU.mult)
-        prep_q("w1", 1, 0, 2)
+        copy_half("w1", 1, 0, "vector")
+        copy_half("w1", 1, 1, "vector")
+        nc.vector.tensor_scalar(out=gate[:], in0=gate_sig[:], scalar1=0.25, scalar2=None, op0=ALU.mult)
+        quantise_halves("w1", 1, 0, 2)
 
-        extra = {}
+        later = [("w2", 0, ps_s2, 0, 1), ("w1", 2, ps_tr, 0, 1), ("w1", 3, ps_tr, 1, 2)]
+        later = later + [("h", c, ps_tr, SUB * c - 3, SUB * c - 1) for c in range(1, NCHUNK)]
 
-        def add(i, place, item):
-            extra[(i, place)] = extra.get((i, place), []) + [item]
-
-        add(0, "pe", ("T", "w2", 0, 0, ps_s2))
-        add(0, "pe", ("T", "w2", 0, 1, ps_s2))
-        add(0, "pe", ("T", "w1", 2, 0, ps_tr))
-        add(0, "pe", ("T", "w1", 2, 1, ps_tr))
-        add(1, "s", ("X", "w2", 0, 0, "S"))
-        add(1, "s", ("X", "w2", 0, 1, "S"))
-        add(1, "s", ("X", "w1", 2, 0, "S"))
-        add(1, "s", ("X", "w1", 2, 1, "S"))
-        add(1, "v2", ("Q", "w2", 0, 0, 2))
-        add(1, "v2", ("Q", "w1", 2, 0, 2))
-        add(1, "pe", ("T", "w1", 3, 0, ps_tr))
-        add(1, "pe", ("T", "w1", 3, 1, ps_tr))
-        add(2, "s", ("X", "w1", 3, 0, "S"))
-        add(2, "s", ("X", "w1", 3, 1, "S"))
-        add(2, "v2", ("Q", "w1", 3, 0, 2))
-        for c in range(1, NCHUNK):
-            f = first_step[c]
-            add(f - 4, "pe", ("T", "h", c, 0, ps_tr))
-            add(f - 4, "pe", ("T", "h", c, 1, ps_tr))
-            add(f - 3, "s", ("X", "h", c, 0, "S"))
-            add(f - 3, "s", ("X", "h", c, 1, "S"))
-            add(f - 3, "v2", ("Q", "h", c, 0, 2))
-
-        def run(i, place):
-            for op, kind, n, x, y in extra.get((i, place), []):
-                if op == "T":
-                    prep_t(kind, n, x, y)
-                elif op == "X":
-                    prep_x(kind, n, x, y)
-                else:
-                    prep_q(kind, n, x, y)
-
-        LAG0 = 2
-
-        def due(i):
-            if i < LAG0:
-                return []
-            if i == LAG0:
-                return list(range(0, LAG0))
-            return [i - 1]
-
-        for i in range(nstep + 1):
+        for i in range(nstep + 4):
+            if 0 <= i - 2 < nstep:
+                stage2(i - 2)
             if i < nstep:
-                for t in range(4):
+                for t in range(PACK):
                     exit1(i, t)
-                    run(i, t)
                     if i + 1 < nstep:
                         stage1(i + 1, t)
-                regroup(i, "S")
-            pend = due(i)
-            for j in pend:
-                stage2(j)
-            run(i, "pe")
-            run(i, "s")
-            run(i, "v0")
-            if i < nstep:
-                regroup(i, "V")
-            run(i, "v1")
+                if by_scalar(i):
+                    regroup(i)
+            for kind, n, pool, i_transpose, i_quantise in later:
+                if i == i_transpose:
+                    transpose_half(kind, n, 0, pool)
+                    transpose_half(kind, n, 1, pool)
+            for kind, n, pool, i_transpose, i_quantise in later:
+                if i == i_transpose + 1:
+                    copy_half(kind, n, 0, "scalar")
+                    copy_half(kind, n, 1, "scalar")
+            if 0 <= i - 1 < nstep and not by_scalar(i - 1):
+                regroup(i - 1)
             if i == 1:
-                nc.vector.tensor_copy(out=b2f[:].rearrange("p e a -> p (e a)"), in_=b2_bf[:])
-            if len(pend) > 0:
-                y_exit(pend[0])
-            if i < nstep:
-                quant1(i)
-            run(i, "v2")
-            for n, j in enumerate(pend):
-                c, s0, ns, e = steps[j]
-                if n > 0:
-                    y_exit(j)
+                nc.vector.tensor_copy(out=b2[:].rearrange("p e a -> p (e a)"), in_=b2_bf[:])
+            if 0 <= i - 3 < nstep:
+                add_b2(i - 3)
+            if 0 <= i - 1 < nstep:
+                quantise_h1(i - 1)
+            for kind, n, pool, i_transpose, i_quantise in later:
+                if i == i_quantise:
+                    quantise_halves(kind, n, 0, 2)
+            if 0 <= i - 3 < nstep:
+                c, s0, ns, e = steps[i - 3]
                 if e == NEXP - 1:
                     store_y(c, s0, ns)
-                gate_acc(j)
+                add_gated(i - 3)
                 if e == NEXP - 1:
                     store_q(c, s0, ns)

@@ -48,7 +48,6 @@ def tile_mspagent_pb_t_kernel(tc, h, gate_logit, e_w1, e_b1, e_w2, e_b2, out_0, 
         ps_s1 = ctx.enter_context(tc.psum_pool(name="ps_s1", bufs=4))
         ps_s2 = ctx.enter_context(tc.psum_pool(name="ps_s2", bufs=2))
         ps_tr = ctx.enter_context(tc.psum_pool(name="ps_tr", bufs=2))
-        ctx.enter_context(tc.manual_schedule())
 
         h_sb = const.tile([P, R * H], BF16, name="h_sb")
         w1_sb = const.tile([P, NEXP * PACK * H], BF16, name="w1_sb")

@@ -22,6 +22,10 @@ SUB = 4
 NCHUNK = R // SUB
 CHUNK = SUB * P
 WORDS = H // 2
+HALF = CHUNK // 2
+
+SCALAR_REGROUPS_EVERY = 12
+SCALAR_REGROUPS_LAST = 3
 
 FLOPS = 2 * M * H * H * NEXP + 2 * M * H * NACT * NEXP
 
@@ -100,7 +104,7 @@ def tile_mspagent_pb_t_kernel(tc, h, gate_logit, e_w1, e_b1, e_w2, e_b2, out_0, 
         w1_words = w1_sb[:].bitcast(F32)
         w2_words = w2_sb[:].bitcast(F32).rearrange("a (e p u) -> a e u p", e=NEXP, u=2)
 
-        def block_words(kind, n, j, u):
+        def tile_words(kind, n, j, u):
             if kind == "h":
                 first = (SUB * n + j) * WORDS + P * u
                 return h_words[:, first : first + P]
@@ -117,13 +121,13 @@ def tile_mspagent_pb_t_kernel(tc, h, gate_logit, e_w1, e_b1, e_w2, e_b2, out_0, 
             bank = pool.tile([P, 2, 2, P], F32, name="tr", tag="bank")
             for j in range(2):
                 for u in range(2):
-                    nc.tensor.transpose(bank[:, j, u, :], block_words(kind, n, 2 * half + j, u), ident[:])
+                    nc.tensor.transpose(bank[:, j, u, :], tile_words(kind, n, 2 * half + j, u), ident[:])
             bank_of[(kind, n, half)] = bank
 
         def copy_half(kind, n, half, engine):
             if (kind, n) not in grouped_of:
-                grouped_of[(kind, n)] = work.tile([P, PACK * P * PACK], BF16, name="grouped", tag="grouped", bufs=4, align_bytes=64)
-            dst = grouped_of[(kind, n)][:].bitcast(F32)[:, 512 * half : 512 * (half + 1)]
+                grouped_of[(kind, n)] = work.tile([P, CHUNK * PACK], BF16, name="grouped", tag="grouped", bufs=4, align_bytes=64)
+            dst = grouped_of[(kind, n)][:].bitcast(F32)[:, 2 * HALF * half : 2 * HALF * (half + 1)]
             dst = dst.rearrange("p (j c u) -> p j c u", j=2, u=2)
             src = bank_of[(kind, n, half)][:].rearrange("p j u c -> p j c u")
             if engine == "scalar":
@@ -134,9 +138,9 @@ def tile_mspagent_pb_t_kernel(tc, h, gate_logit, e_w1, e_b1, e_w2, e_b2, out_0, 
         def quantise_halves(kind, n, lo, hi):
             codes, scales = quantised[kind]
             nc.vector.quantize_mx(
-                out=codes[:, n, 256 * lo : 256 * hi].bitcast(FP8X4),
-                scales=scales[:, n, 256 * lo : 256 * hi],
-                in_=grouped_of[(kind, n)][:, 1024 * lo : 1024 * hi],
+                out=codes[:, n, HALF * lo : HALF * hi].bitcast(FP8X4),
+                scales=scales[:, n, HALF * lo : HALF * hi],
+                in_=grouped_of[(kind, n)][:, PACK * HALF * lo : PACK * HALF * hi],
             )
 
         acc1_of = {}
@@ -174,7 +178,7 @@ def tile_mspagent_pb_t_kernel(tc, h, gate_logit, e_w1, e_b1, e_w2, e_b2, out_0, 
             )
 
         def by_scalar(i):
-            return (i > 0 and i % 12 == 0) or i >= nstep - 2
+            return (i > 0 and i % SCALAR_REGROUPS_EVERY == 0) or i >= nstep - SCALAR_REGROUPS_LAST
 
         def regroup(i):
             c, s0, ns, e = steps[i]
@@ -213,6 +217,9 @@ def tile_mspagent_pb_t_kernel(tc, h, gate_logit, e_w1, e_b1, e_w2, e_b2, out_0, 
                 )
             acc2_of[i] = acc2
 
+        out1_rows = out_1.rearrange("(p r) e a -> p r e a", r=R)
+        out0_rows = out_0.rearrange("(p r) a -> p r a", r=R)
+
         def add_b2(i):
             c, s0, ns, e = steps[i]
             if c not in y_of:
@@ -223,6 +230,10 @@ def tile_mspagent_pb_t_kernel(tc, h, gate_logit, e_w1, e_b1, e_w2, e_b2, out_0, 
                 in1=b2[:, e, :].unsqueeze(1).to_broadcast([P, ns, NACT]),
                 op=ALU.add,
             )
+
+        def store_y(i):
+            c, s0, ns, e = steps[i]
+            nc.sync.dma_start(out=out1_rows[:, SUB * c + s0 : SUB * c + s0 + ns, e, :], in_=y_of[c][:, s0 : s0 + ns, e, :])
 
         def add_gated(i):
             c, s0, ns, e = steps[i]
@@ -237,16 +248,8 @@ def tile_mspagent_pb_t_kernel(tc, h, gate_logit, e_w1, e_b1, e_w2, e_b2, out_0, 
                         out=q_of[c][:, s, :], in0=y_of[c][:, s, e, :], scalar=g, in1=q_of[c][:, s, :], op0=ALU.mult, op1=ALU.add
                     )
 
-        out1_rows = out_1.rearrange("(p r) e a -> p r (e a)", r=R)
-        out0_rows = out_0.rearrange("(p r) a -> p r a", r=R)
-
-        def store_y(c, s0, ns):
-            nc.sync.dma_start(
-                out=out1_rows[:, SUB * c + s0 : SUB * c + s0 + ns, :],
-                in_=y_of[c][:, s0 : s0 + ns, :, :].rearrange("p s e a -> p s (e a)"),
-            )
-
-        def store_q(c, s0, ns):
+        def store_q(i):
+            c, s0, ns, e = steps[i]
             nc.sync.dma_start(out=out0_rows[:, SUB * c + s0 : SUB * c + s0 + ns, :], in_=q_of[c][:, s0 : s0 + ns, :])
 
         transpose_half("h", 0, 0, ps_tr)
@@ -270,7 +273,7 @@ def tile_mspagent_pb_t_kernel(tc, h, gate_logit, e_w1, e_b1, e_w2, e_b2, out_0, 
         stage1(0, 3)
         copy_half("w1", 1, 0, "vector")
         copy_half("w1", 1, 1, "vector")
-        nc.vector.tensor_scalar(out=gate[:], in0=gate_sig[:], scalar1=0.25, scalar2=None, op0=ALU.mult)
+        nc.vector.tensor_scalar(out=gate[:], in0=gate_sig[:], scalar1=1.0 / NEXP, scalar2=None, op0=ALU.mult)
         quantise_halves("w1", 1, 0, 2)
 
         later = [("w2", 0, ps_s2, 0, 1), ("w1", 2, ps_tr, 0, 1), ("w1", 3, ps_tr, 1, 2)]
@@ -300,15 +303,13 @@ def tile_mspagent_pb_t_kernel(tc, h, gate_logit, e_w1, e_b1, e_w2, e_b2, out_0, 
                 nc.vector.tensor_copy(out=b2[:].rearrange("p e a -> p (e a)"), in_=b2_bf[:])
             if 0 <= i - 3 < nstep:
                 add_b2(i - 3)
+                store_y(i - 3)
             if 0 <= i - 1 < nstep:
                 quantise_h1(i - 1)
             for kind, n, pool, i_transpose, i_quantise in later:
                 if i == i_quantise:
                     quantise_halves(kind, n, 0, 2)
             if 0 <= i - 3 < nstep:
-                c, s0, ns, e = steps[i - 3]
-                if e == NEXP - 1:
-                    store_y(c, s0, ns)
                 add_gated(i - 3)
-                if e == NEXP - 1:
-                    store_q(c, s0, ns)
+                if steps[i - 3][3] == NEXP - 1:
+                    store_q(i - 3)

@@ -183,8 +183,8 @@ def tile_mspagent_pb_t_kernel(tc, h, gate_logit, e_w1, e_b1, e_w2, e_b2, out_0, 
         def regroup(i):
             c, s0, ns, e = steps[i]
             packed_of[i] = work.tile([P, CHUNK, PACK], BF16, name="packed", tag="packed", bufs=3, align_bytes=64)
-            dst = packed_of[i][:, : P * ns, :].rearrange("p (c i) t -> p c t i", i=4)
-            src = planes_of[i][:, :, : P * ns].rearrange("p t (c i) -> p c t i", i=4)
+            dst = packed_of[i][:, : P * ns, :].rearrange("p (c i) t -> p c t i", i=8)
+            src = planes_of[i][:, :, : P * ns].rearrange("p t (c i) -> p c t i", i=8)
             if by_scalar(i):
                 nc.scalar.copy(out=dst, in_=src)
             else:

@@ -58,7 +58,10 @@ def tile_mspagent_pb_t_kernel(tc, h, gate_logit, e_w1, e_b1, e_w2, e_b2, out_0, 
         w2_sb = const.tile([P, NEXP * H], BF16, name="w2_sb")
         b1_bf = const.tile([P, NEXP, PACK], BF16, name="b1_bf")
         b1 = const.tile([P, NEXP * PACK], F32, name="b1")
-        b2_bf = const.tile([P, NEXP * NACT], BF16, name="b2_bf")
+        b2_row = const.tile([P, NEXP * NACT], BF16, name="b2_row")
+        ones = const.tile([P, P], BF16, name="ones")
+        table_in = const.tile([P, 1], F32, name="table_in")
+        table_out = const.tile([P, 1], F32, name="table_out")
         b2 = const.tile([P, NEXP, NACT], F32, name="b2")
         gate_bf = const.tile([P, R * NEXP], BF16, name="gate_bf")
         gate_sig = const.tile([P, R * NEXP], F32, name="gate_sig")
@@ -83,22 +86,25 @@ def tile_mspagent_pb_t_kernel(tc, h, gate_logit, e_w1, e_b1, e_w2, e_b2, out_0, 
                 in_=e_w1[e].rearrange("(p t) k -> p (t k)", t=PACK)[:, lo * H : hi * H],
             )
 
-        nc.scalar.dma_start(out=gate_bf[:], in_=gate_logit.rearrange("(p r) e -> p (r e)", r=R))
-        nc.scalar.dma_start(out=b1_bf[:], in_=e_b1.rearrange("e (p t) -> p e t", t=PACK))
+        nc.gpsimd.memset(table_in[:], 0.0)
+        nc.scalar.activation(out=table_out[:], in_=table_in[:], func=ACT.Sigmoid)
+        nc.gpsimd.memset(b2_row[:].bitcast(F32), 0.0)
+        nc.gpsimd.memset(ones[:], 1.0)
         load_h(0, 0, 2)
         load_w1(0, 0, 2)
         load_h(0, 2, 4)
         load_w1(0, 2, 4)
+        nc.sync.dma_start(out=b1_bf[:], in_=e_b1.rearrange("e (p t) -> p e t", t=PACK))
         load_w1(1, 0, 4)
+        nc.sync.dma_start(out=gate_bf[:], in_=gate_logit.rearrange("(p r) e -> p (r e)", r=R))
+        nc.sync.dma_start(out=b2_row[:1, :], in_=e_b2.rearrange("e a -> (e a)").unsqueeze(0))
         nc.sync.dma_start(out=w2_sb[:].rearrange("a (e k) -> a e k", e=NEXP), in_=e_w2.rearrange("e a k -> a e k"))
         load_w1(2, 0, 4)
         load_w1(3, 0, 4)
-        nc.scalar.dma_start(out=b2_bf[:], in_=e_b2.rearrange("e a -> (e a)").partition_broadcast(P))
         for c in range(1, NCHUNK):
             load_h(c, 0, 4)
 
         make_identity(nc, ident[:])
-        nc.scalar.activation(out=gate_sig[:], in_=gate_bf[:], func=ACT.Sigmoid)
 
         h_words = h_sb[:].bitcast(F32)
         w1_words = w1_sb[:].bitcast(F32)
@@ -273,7 +279,6 @@ def tile_mspagent_pb_t_kernel(tc, h, gate_logit, e_w1, e_b1, e_w2, e_b2, out_0, 
         stage1(0, 3)
         copy_half("w1", 1, 0, "vector")
         copy_half("w1", 1, 1, "vector")
-        nc.vector.tensor_scalar(out=gate[:], in0=gate_sig[:], scalar1=1.0 / NEXP, scalar2=None, op0=ALU.mult)
         quantise_halves("w1", 1, 0, 2)
 
         later = [("w2", 0, ps_s2, 0, 1), ("w1", 2, ps_tr, 0, 1), ("w1", 3, ps_tr, 1, 2)]
@@ -300,7 +305,11 @@ def tile_mspagent_pb_t_kernel(tc, h, gate_logit, e_w1, e_b1, e_w2, e_b2, out_0, 
             if 0 <= i - 1 < nstep and not by_scalar(i - 1):
                 regroup(i - 1)
             if i == 1:
-                nc.vector.tensor_copy(out=b2[:].rearrange("p e a -> p (e a)"), in_=b2_bf[:])
+                b2_bank = ps_tr.tile([P, NEXP * NACT], F32, name="b2_bank", tag="bank")
+                nc.tensor.matmul(b2_bank[:], lhsT=ones[:], rhs=b2_row[:], start=True, stop=True)
+                nc.vector.tensor_copy(out=b2[:].rearrange("p e a -> p (e a)"), in_=b2_bank[:])
+                nc.scalar.activation(out=gate_sig[:], in_=gate_bf[:], func=ACT.Sigmoid)
+                nc.vector.tensor_scalar(out=gate[:], in0=gate_sig[:], scalar1=1.0 / NEXP, scalar2=None, op0=ALU.mult)
             if 0 <= i - 3 < nstep:
                 add_b2(i - 3)
                 store_y(i - 3)

@@ -86,6 +86,7 @@ def tile_mspagent_pb_t_kernel(tc, h, gate_logit, e_w1, e_b1, e_w2, e_b2, out_0, 
                 in_=e_w1[e].rearrange("(p t) k -> p (t k)", t=PACK)[:, lo * H : hi * H],
             )
 
+        nc.scalar.dma_start(out=gate_bf[:], in_=gate_logit.rearrange("(p r) e -> p (r e)", r=R))
         nc.gpsimd.memset(table_in[:], 0.0)
         nc.scalar.activation(out=table_out[:], in_=table_in[:], func=ACT.Sigmoid)
         nc.gpsimd.memset(b2_row[:].bitcast(F32), 0.0)
@@ -96,7 +97,6 @@ def tile_mspagent_pb_t_kernel(tc, h, gate_logit, e_w1, e_b1, e_w2, e_b2, out_0, 
         load_w1(0, 2, 4)
         nc.sync.dma_start(out=b1_bf[:], in_=e_b1.rearrange("e (p t) -> p e t", t=PACK))
         load_w1(1, 0, 4)
-        nc.sync.dma_start(out=gate_bf[:], in_=gate_logit.rearrange("(p r) e -> p (r e)", r=R))
         nc.sync.dma_start(out=b2_row[:1, :], in_=e_b2.rearrange("e a -> (e a)").unsqueeze(0))
         nc.sync.dma_start(out=w2_sb[:].rearrange("a (e k) -> a e k", e=NEXP), in_=e_w2.rearrange("e a k -> a e k"))
         load_w1(2, 0, 4)
@@ -300,8 +300,9 @@ def tile_mspagent_pb_t_kernel(tc, h, gate_logit, e_w1, e_b1, e_w2, e_b2, out_0, 
                     transpose_half(kind, n, 1, pool)
             for kind, n, pool, i_transpose, i_quantise in later:
                 if i == i_transpose + 1:
-                    copy_half(kind, n, 0, "scalar")
-                    copy_half(kind, n, 1, "scalar")
+                    engine = "vector" if kind == "w2" else "scalar"
+                    copy_half(kind, n, 0, engine)
+                    copy_half(kind, n, 1, engine)
             if 0 <= i - 1 < nstep and not by_scalar(i - 1):
                 regroup(i - 1)
             if i == 1:

@@ -87,6 +87,7 @@ def tile_mspagent_pb_t_kernel(tc, h, gate_logit, e_w1, e_b1, e_w2, e_b2, out_0, 
             )
 
         nc.scalar.dma_start(out=gate_bf[:], in_=gate_logit.rearrange("(p r) e -> p (r e)", r=R))
+        nc.scalar.dma_start(out=b1_bf[:], in_=e_b1.rearrange("e (p t) -> p e t", t=PACK))
         nc.gpsimd.memset(table_in[:], 0.0)
         nc.scalar.activation(out=table_out[:], in_=table_in[:], func=ACT.Sigmoid)
         nc.gpsimd.memset(b2_row[:].bitcast(F32), 0.0)
@@ -95,9 +96,8 @@ def tile_mspagent_pb_t_kernel(tc, h, gate_logit, e_w1, e_b1, e_w2, e_b2, out_0, 
         load_w1(0, 0, 2)
         load_h(0, 2, 4)
         load_w1(0, 2, 4)
-        nc.sync.dma_start(out=b1_bf[:], in_=e_b1.rearrange("e (p t) -> p e t", t=PACK))
-        load_w1(1, 0, 4)
         nc.sync.dma_start(out=b2_row[:1, :], in_=e_b2.rearrange("e a -> (e a)").unsqueeze(0))
+        load_w1(1, 0, 4)
         nc.sync.dma_start(out=w2_sb[:].rearrange("a (e k) -> a e k", e=NEXP), in_=e_w2.rearrange("e a k -> a e k"))
         load_w1(2, 0, 4)
         load_w1(3, 0, 4)
@@ -105,6 +105,9 @@ def tile_mspagent_pb_t_kernel(tc, h, gate_logit, e_w1, e_b1, e_w2, e_b2, out_0, 
             load_h(c, 0, 4)
 
         make_identity(nc, ident[:])
+        nc.gpsimd.tensor_copy(out=b1[:], in_=b1_bf[:].rearrange("p e t -> p (e t)"))
+        nc.scalar.activation(out=gate_sig[:], in_=gate_bf[:], func=ACT.Sigmoid)
+        nc.gpsimd.tensor_scalar(out=gate[:], in0=gate_sig[:], scalar1=1.0 / NEXP, scalar2=None, op0=ALU.mult)
 
         h_words = h_sb[:].bitcast(F32)
         w1_words = w1_sb[:].bitcast(F32)
@@ -267,7 +270,9 @@ def tile_mspagent_pb_t_kernel(tc, h, gate_logit, e_w1, e_b1, e_w2, e_b2, out_0, 
         copy_half("h", 0, 1, "scalar")
         quantise_halves("w1", 0, 0, 1)
         transpose_half("w1", 0, 1, ps_s2)
-        nc.vector.tensor_copy(out=b1[:], in_=b1_bf[:].rearrange("p e t -> p (e t)"))
+        b2_bank = ps_tr.tile([P, NEXP * NACT], F32, name="b2_bank", tag="bank")
+        nc.tensor.matmul(b2_bank[:], lhsT=ones[:], rhs=b2_row[:], start=True, stop=True)
+        nc.scalar.copy(out=b2[:].rearrange("p e a -> p (e a)"), in_=b2_bank[:])
         copy_half("w1", 0, 1, "vector")
         stage1(0, 0)
         stage1(0, 1)
@@ -305,12 +310,6 @@ def tile_mspagent_pb_t_kernel(tc, h, gate_logit, e_w1, e_b1, e_w2, e_b2, out_0, 
                     copy_half(kind, n, 1, engine)
             if 0 <= i - 1 < nstep and not by_scalar(i - 1):
                 regroup(i - 1)
-            if i == 1:
-                b2_bank = ps_tr.tile([P, NEXP * NACT], F32, name="b2_bank", tag="bank")
-                nc.tensor.matmul(b2_bank[:], lhsT=ones[:], rhs=b2_row[:], start=True, stop=True)
-                nc.vector.tensor_copy(out=b2[:].rearrange("p e a -> p (e a)"), in_=b2_bank[:])
-                nc.scalar.activation(out=gate_sig[:], in_=gate_bf[:], func=ACT.Sigmoid)
-                nc.vector.tensor_scalar(out=gate[:], in0=gate_sig[:], scalar1=1.0 / NEXP, scalar2=None, op0=ALU.mult)
             if 0 <= i - 3 < nstep:
                 add_b2(i - 3)
                 store_y(i - 3)

@@ -86,17 +86,17 @@ def tile_mspagent_pb_t_kernel(tc, h, gate_logit, e_w1, e_b1, e_w2, e_b2, out_0, 
                 in_=e_w1[e].rearrange("(p t) k -> p (t k)", t=PACK)[:, lo * H : hi * H],
             )
 
-        nc.scalar.dma_start(out=gate_bf[:], in_=gate_logit.rearrange("(p r) e -> p (r e)", r=R))
-        nc.scalar.dma_start(out=b1_bf[:], in_=e_b1.rearrange("e (p t) -> p e t", t=PACK))
         nc.gpsimd.memset(table_in[:], 0.0)
         nc.scalar.activation(out=table_out[:], in_=table_in[:], func=ACT.Sigmoid)
         nc.gpsimd.memset(b2_row[:].bitcast(F32), 0.0)
+        nc.scalar.dma_start(out=b2_row[:1, :], in_=e_b2.rearrange("e a -> (e a)").unsqueeze(0))
         nc.gpsimd.memset(ones[:], 1.0)
         load_h(0, 0, 2)
         load_w1(0, 0, 2)
         load_h(0, 2, 4)
         load_w1(0, 2, 4)
-        nc.sync.dma_start(out=b2_row[:1, :], in_=e_b2.rearrange("e a -> (e a)").unsqueeze(0))
+        nc.sync.dma_start(out=b1_bf[:], in_=e_b1.rearrange("e (p t) -> p e t", t=PACK))
+        nc.sync.dma_start(out=gate_bf[:], in_=gate_logit.rearrange("(p r) e -> p (r e)", r=R))
         load_w1(1, 0, 4)
         nc.sync.dma_start(out=w2_sb[:].rearrange("a (e k) -> a e k", e=NEXP), in_=e_w2.rearrange("e a k -> a e k"))
         load_w1(2, 0, 4)
@@ -106,8 +106,6 @@ def tile_mspagent_pb_t_kernel(tc, h, gate_logit, e_w1, e_b1, e_w2, e_b2, out_0, 
 
         make_identity(nc, ident[:])
         nc.gpsimd.tensor_copy(out=b1[:], in_=b1_bf[:].rearrange("p e t -> p (e t)"))
-        nc.scalar.activation(out=gate_sig[:], in_=gate_bf[:], func=ACT.Sigmoid)
-        nc.gpsimd.tensor_scalar(out=gate[:], in0=gate_sig[:], scalar1=1.0 / NEXP, scalar2=None, op0=ALU.mult)
 
         h_words = h_sb[:].bitcast(F32)
         w1_words = w1_sb[:].bitcast(F32)
@@ -261,30 +259,33 @@ def tile_mspagent_pb_t_kernel(tc, h, gate_logit, e_w1, e_b1, e_w2, e_b2, out_0, 
             c, s0, ns, e = steps[i]
             nc.sync.dma_start(out=out0_rows[:, SUB * c + s0 : SUB * c + s0 + ns, :], in_=q_of[c][:, s0 : s0 + ns, :])
 
-        transpose_half("h", 0, 0, ps_tr)
-        copy_half("h", 0, 0, "scalar")
-        transpose_half("w1", 0, 0, ps_s2)
-        copy_half("w1", 0, 0, "vector")
-        quantise_halves("h", 0, 0, 1)
-        transpose_half("h", 0, 1, ps_tr)
-        copy_half("h", 0, 1, "scalar")
-        quantise_halves("w1", 0, 0, 1)
-        transpose_half("w1", 0, 1, ps_s2)
-        b2_bank = ps_tr.tile([P, NEXP * NACT], F32, name="b2_bank", tag="bank")
-        nc.tensor.matmul(b2_bank[:], lhsT=ones[:], rhs=b2_row[:], start=True, stop=True)
-        nc.scalar.copy(out=b2[:].rearrange("p e a -> p (e a)"), in_=b2_bank[:])
-        copy_half("w1", 0, 1, "vector")
-        stage1(0, 0)
-        stage1(0, 1)
-        transpose_half("w1", 1, 0, ps_tr)
-        transpose_half("w1", 1, 1, ps_tr)
-        quantise_halves("w1", 0, 1, 2)
-        quantise_halves("h", 0, 1, 2)
-        stage1(0, 2)
-        stage1(0, 3)
-        copy_half("w1", 1, 0, "vector")
-        copy_half("w1", 1, 1, "vector")
-        quantise_halves("w1", 1, 0, 2)
+        with tc.manual_schedule(engines={mybir.EngineType.Activation}):
+            transpose_half("h", 0, 0, ps_tr)
+            copy_half("h", 0, 0, "scalar")
+            transpose_half("w1", 0, 0, ps_s2)
+            copy_half("w1", 0, 0, "vector")
+            quantise_halves("h", 0, 0, 1)
+            transpose_half("h", 0, 1, ps_tr)
+            copy_half("h", 0, 1, "scalar")
+            quantise_halves("w1", 0, 0, 1)
+            transpose_half("w1", 0, 1, ps_s2)
+            b2_bank = ps_tr.tile([P, NEXP * NACT], F32, name="b2_bank", tag="bank")
+            nc.tensor.matmul(b2_bank[:], lhsT=ones[:], rhs=b2_row[:], start=True, stop=True)
+            nc.scalar.copy(out=b2[:].rearrange("p e a -> p (e a)"), in_=b2_bank[:])
+            copy_half("w1", 0, 1, "vector")
+            stage1(0, 0)
+            stage1(0, 1)
+            transpose_half("w1", 1, 0, ps_tr)
+            transpose_half("w1", 1, 1, ps_tr)
+            quantise_halves("w1", 0, 1, 2)
+            quantise_halves("h", 0, 1, 2)
+            stage1(0, 2)
+            stage1(0, 3)
+            copy_half("w1", 1, 0, "vector")
+            copy_half("w1", 1, 1, "vector")
+            quantise_halves("w1", 1, 0, 2)
+            nc.scalar.activation(out=gate_sig[:], in_=gate_bf[:], func=ACT.Sigmoid)
+            nc.gpsimd.tensor_scalar(out=gate[:], in0=gate_sig[:], scalar1=1.0 / NEXP, scalar2=0.0, op0=ALU.mult, op1=ALU.add)
 
         later = [("w2", 0, ps_s2, 0, 1), ("w1", 2, ps_tr, 0, 1), ("w1", 3, ps_tr, 1, 2)]
         later = later + [("h", c, ps_tr, SUB * c - 3, SUB * c - 1) for c in range(1, NCHUNK)]

from contextlib import ExitStack

import concourse.mybir as mybir
from concourse.masks import make_identity

F32 = mybir.dt.float32
BF16 = mybir.dt.bfloat16
U32 = mybir.dt.uint32
U8 = mybir.dt.uint8
FP8X4 = mybir.dt.float8_e4m3fn_x4
ACT = mybir.ActivationFunctionType
ALU = mybir.AluOpType

P = 128
PACK = 4
M = 4096
H = 512
NEXP = 4
NACT = 128
R = M // P
SUB = 4
NCHUNK = R // SUB
CHUNK = SUB * P
WORDS = H // 2
HALF = CHUNK // 2

SCALAR_REGROUPS_EVERY = 12
SCALAR_REGROUPS_LAST = 3

FLOPS = 2 * M * H * H * NEXP + 2 * M * H * NACT * NEXP


def step_list():
    steps = []
    for c in range(NCHUNK):
        for e in range(NEXP):
            if (c == 0 and e == 0) or (c == NCHUNK - 1 and e == NEXP - 1):
                steps.append((c, 0, SUB // 2, e))
                steps.append((c, SUB // 2, SUB // 2, e))
            else:
                steps.append((c, 0, SUB, e))
    return steps


def tile_mspagent_pb_t_kernel(tc, h, gate_logit, e_w1, e_b1, e_w2, e_b2, out_0, out_1):
    nc = tc.nc
    steps = step_list()
    nstep = len(steps)
    with ExitStack() as ctx:
        const = ctx.enter_context(tc.tile_pool(name="const", bufs=1))
        work = ctx.enter_context(tc.tile_pool(name="work", bufs=2))
        ps_s1 = ctx.enter_context(tc.psum_pool(name="ps_s1", bufs=4))
        ps_s2 = ctx.enter_context(tc.psum_pool(name="ps_s2", bufs=2))
        ps_tr = ctx.enter_context(tc.psum_pool(name="ps_tr", bufs=2))

        h_sb = const.tile([P, R * H], BF16, name="h_sb")
        w1_sb = const.tile([P, NEXP * PACK * H], BF16, name="w1_sb")
        w2_sb = const.tile([P, NEXP * H], BF16, name="w2_sb")
        b1_bf = const.tile([P, NEXP, PACK], BF16, name="b1_bf")
        b1 = const.tile([P, NEXP * PACK], F32, name="b1")
        b2_row = const.tile([P, NEXP * NACT], BF16, name="b2_row")
        ones = const.tile([P, P], BF16, name="ones")
        table_in = const.tile([P, 1], F32, name="table_in")
        table_out = const.tile([P, 1], F32, name="table_out")
        b2 = const.tile([P, NEXP, NACT], F32, name="b2")
        gate_bf = const.tile([P, R * NEXP], BF16, name="gate_bf")
        gate_sig = const.tile([P, R * NEXP], F32, name="gate_sig")
        gate = const.tile([P, R * NEXP], F32, name="gate")
        ident = const.tile([P, P], F32, name="ident")
        h_codes = const.tile([P, NCHUNK, CHUNK], U32, name="h_codes", align_bytes=64)
        h_scales = const.tile([P, NCHUNK, CHUNK], U8, name="h_scales", align_bytes=64)
        w1_codes = const.tile([P, NEXP, PACK * P], U32, name="w1_codes", align_bytes=64)
        w1_scales = const.tile([P, NEXP, PACK * P], U8, name="w1_scales", align_bytes=64)
        w2_codes = const.tile([P, 1, NEXP * NACT], U32, name="w2_codes", align_bytes=64)
        w2_scales = const.tile([P, 1, NEXP * NACT], U8, name="w2_scales", align_bytes=64)

        h_rows = h.rearrange("(p r) k -> p (r k)", r=R)

        def load_h(c, lo, hi):
            cols = slice((SUB * c + lo) * H, (SUB * c + hi) * H)
            nc.sync.dma_start(out=h_sb[:, cols], in_=h_rows[:, cols])

        def load_w1(e, lo, hi):
            nc.sync.dma_start(
                out=w1_sb[:, (PACK * e + lo) * H : (PACK * e + hi) * H],
                in_=e_w1[e].rearrange("(p t) k -> p (t k)", t=PACK)[:, lo * H : hi * H],
            )

        nc.gpsimd.memset(table_in[:], 0.0)
        nc.scalar.activation(out=table_out[:], in_=table_in[:], func=ACT.Sigmoid)
        nc.gpsimd.memset(b2_row[:].bitcast(F32), 0.0)
        nc.scalar.dma_start(out=b2_row[:1, :], in_=e_b2.rearrange("e a -> (e a)").unsqueeze(0))
        nc.gpsimd.memset(ones[:], 1.0)
        load_h(0, 0, 2)
        load_w1(0, 0, 2)
        load_h(0, 2, 4)
        load_w1(0, 2, 4)
        nc.sync.dma_start(out=b1_bf[:], in_=e_b1.rearrange("e (p t) -> p e t", t=PACK))
        nc.sync.dma_start(out=gate_bf[:], in_=gate_logit.rearrange("(p r) e -> p (r e)", r=R))
        load_w1(1, 0, 4)
        nc.sync.dma_start(out=w2_sb[:].rearrange("a (e k) -> a e k", e=NEXP), in_=e_w2.rearrange("e a k -> a e k"))
        load_w1(2, 0, 4)
        load_w1(3, 0, 4)
        for c in range(1, NCHUNK):
            load_h(c, 0, 4)

        make_identity(nc, ident[:])
        nc.gpsimd.tensor_copy(out=b1[:], in_=b1_bf[:].rearrange("p e t -> p (e t)"))

        h_words = h_sb[:].bitcast(F32)
        w1_words = w1_sb[:].bitcast(F32)
        w2_words = w2_sb[:].bitcast(F32).rearrange("a (e p u) -> a e u p", e=NEXP, u=2)

        def tile_words(kind, n, j, u):
            if kind == "h":
                first = (SUB * n + j) * WORDS + P * u
                return h_words[:, first : first + P]
            if kind == "w1":
                first = (PACK * n + j) * WORDS + P * u
                return w1_words[:, first : first + P]
            return w2_words[:, j, u, :]

        quantised = {"h": (h_codes, h_scales), "w1": (w1_codes, w1_scales), "w2": (w2_codes, w2_scales)}
        bank_of = {}
        grouped_of = {}

        def transpose_half(kind, n, half, pool):
            bank = pool.tile([P, 2, 2, P], F32, name="tr", tag="bank")
            for j in range(2):
                for u in range(2):
                    nc.tensor.transpose(bank[:, j, u, :], tile_words(kind, n, 2 * half + j, u), ident[:])
            bank_of[(kind, n, half)] = bank

        def copy_half(kind, n, half, engine):
            if (kind, n) not in grouped_of:
                grouped_of[(kind, n)] = work.tile([P, CHUNK * PACK], BF16, name="grouped", tag="grouped", bufs=4, align_bytes=64)
            dst = grouped_of[(kind, n)][:].bitcast(F32)[:, 2 * HALF * half : 2 * HALF * (half + 1)]
            dst = dst.rearrange("p (j c u) -> p j c u", j=2, u=2)
            src = bank_of[(kind, n, half)][:].rearrange("p j u c -> p j c u")
            if engine == "scalar":
                nc.scalar.copy(out=dst, in_=src)
            else:
                nc.vector.tensor_copy(out=dst, in_=src)

        def quantise_halves(kind, n, lo, hi):
            codes, scales = quantised[kind]
            nc.vector.quantize_mx(
                out=codes[:, n, HALF * lo : HALF * hi].bitcast(FP8X4),
                scales=scales[:, n, HALF * lo : HALF * hi],
                in_=grouped_of[(kind, n)][:, PACK * HALF * lo : PACK * HALF * hi],
            )

        acc1_of = {}
        planes_of = {}
        packed_of = {}
        h1_of = {}
        acc2_of = {}
        y_of = {}
        q_of = {}

        def stage1(i, t):
            c, s0, ns, e = steps[i]
            acc1 = ps_s1.tile([P, CHUNK], F32, name="acc1", tag="bank")
            nc.tensor.matmul_mx(
                out=acc1[:, : P * ns],
                lhsT=w1_codes[:, e, P * t : P * (t + 1)].bitcast(FP8X4),
                lhsT_scale=w1_scales[:, e, P * t : P * (t + 1)],
                rhs=h_codes[:, c, P * s0 : P * (s0 + ns)].bitcast(FP8X4),
                rhs_scale=h_scales[:, c, P * s0 : P * (s0 + ns)],
                start=True,
                stop=True,
            )
            acc1_of[(i, t)] = acc1

        def exit1(i, t):
            c, s0, ns, e = steps[i]
            if t == 0:
                planes_of[i] = work.tile([P, PACK, CHUNK], BF16, name="planes", tag="planes", bufs=4)
            nc.scalar.activation(
                out=planes_of[i][:, t, : P * ns],
                in_=acc1_of[(i, t)][:, : P * ns],
                func=ACT.Relu,
                bias=b1[:, PACK * e + t : PACK * e + t + 1],
                scale=1.0,
            )

        def by_scalar(i):
            return (i > 0 and i % SCALAR_REGROUPS_EVERY == 0) or i >= nstep - SCALAR_REGROUPS_LAST

        def regroup(i):
            c, s0, ns, e = steps[i]
            packed_of[i] = work.tile([P, CHUNK, PACK], BF16, name="packed", tag="packed", bufs=3, align_bytes=64)
            dst = packed_of[i][:, : P * ns, :].rearrange("p (c i) t -> p c t i", i=8)
            src = planes_of[i][:, :, : P * ns].rearrange("p t (c i) -> p c t i", i=8)
            if by_scalar(i):
                nc.scalar.copy(out=dst, in_=src)
            else:
                nc.vector.tensor_copy(out=dst, in_=src)

        def quantise_h1(i):
            c, s0, ns, e = steps[i]
            codes = work.tile([P, CHUNK], U32, name="h1_codes", tag="h1_codes", bufs=4, align_bytes=64)
            scales = work.tile([P, CHUNK], U8, name="h1_scales", tag="h1_scales", bufs=4, align_bytes=64)
            nc.vector.quantize_mx(
                out=codes[:, : P * ns].bitcast(FP8X4),
                scales=scales[:, : P * ns],
                in_=packed_of[i][:, : P * ns, :].rearrange("p c t -> p (c t)"),
            )
            h1_of[i] = (codes, scales)

        def stage2(i):
            c, s0, ns, e = steps[i]
            codes, scales = h1_of[i]
            acc2 = ps_s2.tile([P, SUB, NACT], F32, name="acc2", tag="bank")
            for s in range(ns):
                nc.tensor.matmul_mx(
                    out=acc2[:, s, :],
                    lhsT=codes[:, P * s : P * (s + 1)].bitcast(FP8X4),
                    lhsT_scale=scales[:, P * s : P * (s + 1)],
                    rhs=w2_codes[:, 0, NACT * e : NACT * (e + 1)].bitcast(FP8X4),
                    rhs_scale=w2_scales[:, 0, NACT * e : NACT * (e + 1)],
                    start=True,
                    stop=True,
                )
            acc2_of[i] = acc2

        out1_rows = out_1.rearrange("(p r) e a -> p r e a", r=R)
        out0_rows = out_0.rearrange("(p r) a -> p r a", r=R)

        def add_b2(i):
            c, s0, ns, e = steps[i]
            if c not in y_of:
                y_of[c] = work.tile([P, SUB, NEXP, NACT], F32, name="y", tag="y", bufs=3)
            nc.vector.tensor_tensor(
                out=y_of[c][:, s0 : s0 + ns, e, :],
                in0=acc2_of[i][:, :ns, :],
                in1=b2[:, e, :].unsqueeze(1).to_broadcast([P, ns, NACT]),
                op=ALU.add,
            )

        def store_y(i):
            c, s0, ns, e = steps[i]
            nc.sync.dma_start(out=out1_rows[:, SUB * c + s0 : SUB * c + s0 + ns, e, :], in_=y_of[c][:, s0 : s0 + ns, e, :])

        def add_gated(i):
            c, s0, ns, e = steps[i]
            if c not in q_of:
                q_of[c] = work.tile([P, SUB, NACT], F32, name="q", tag="q", bufs=3)
            for s in range(s0, s0 + ns):
                g = gate[:, (SUB * c + s) * NEXP + e : (SUB * c + s) * NEXP + e + 1]
                if e == 0:
                    nc.vector.tensor_scalar(out=q_of[c][:, s, :], in0=y_of[c][:, s, e, :], scalar1=g, scalar2=None, op0=ALU.mult)
                else:
                    nc.vector.scalar_tensor_tensor(
                        out=q_of[c][:, s, :], in0=y_of[c][:, s, e, :], scalar=g, in1=q_of[c][:, s, :], op0=ALU.mult, op1=ALU.add
                    )

        def store_q(i):
            c, s0, ns, e = steps[i]
            nc.sync.dma_start(out=out0_rows[:, SUB * c + s0 : SUB * c + s0 + ns, :], in_=q_of[c][:, s0 : s0 + ns, :])

        with tc.manual_schedule(engines={mybir.EngineType.Activation}):
            transpose_half("h", 0, 0, ps_tr)
            copy_half("h", 0, 0, "scalar")
            transpose_half("w1", 0, 0, ps_s2)
            copy_half("w1", 0, 0, "vector")
            quantise_halves("h", 0, 0, 1)
            transpose_half("h", 0, 1, ps_tr)
            copy_half("h", 0, 1, "scalar")
            quantise_halves("w1", 0, 0, 1)
            transpose_half("w1", 0, 1, ps_s2)
            b2_bank = ps_tr.tile([P, NEXP * NACT], F32, name="b2_bank", tag="bank")
            nc.tensor.matmul(b2_bank[:], lhsT=ones[:], rhs=b2_row[:], start=True, stop=True)
            nc.scalar.copy(out=b2[:].rearrange("p e a -> p (e a)"), in_=b2_bank[:])
            copy_half("w1", 0, 1, "vector")
            stage1(0, 0)
            stage1(0, 1)
            transpose_half("w1", 1, 0, ps_tr)
            transpose_half("w1", 1, 1, ps_tr)
            quantise_halves("w1", 0, 1, 2)
            quantise_halves("h", 0, 1, 2)
            stage1(0, 2)
            stage1(0, 3)
            copy_half("w1", 1, 0, "vector")
            copy_half("w1", 1, 1, "vector")
            quantise_halves("w1", 1, 0, 2)
            nc.scalar.activation(out=gate_sig[:], in_=gate_bf[:], func=ACT.Sigmoid)
            nc.gpsimd.tensor_scalar(out=gate[:], in0=gate_sig[:], scalar1=1.0 / NEXP, scalar2=0.0, op0=ALU.mult, op1=ALU.add)

        later = [("w2", 0, ps_s2, 0, 1), ("w1", 2, ps_tr, 0, 1), ("w1", 3, ps_tr, 1, 2)]
        later = later + [("h", c, ps_tr, SUB * c - 3, SUB * c - 1) for c in range(1, NCHUNK)]

        for i in range(nstep + 4):
            if 0 <= i - 2 < nstep:
                stage2(i - 2)
            if i < nstep:
                for t in range(PACK):
                    exit1(i, t)
                    if i + 1 < nstep:
                        stage1(i + 1, t)
                if by_scalar(i):
                    regroup(i)
            for kind, n, pool, i_transpose, i_quantise in later:
                if i == i_transpose:
                    transpose_half(kind, n, 0, pool)
                    transpose_half(kind, n, 1, pool)
            for kind, n, pool, i_transpose, i_quantise in later:
                if i == i_transpose + 1:
                    engine = "vector" if kind == "w2" else "scalar"
                    copy_half(kind, n, 0, engine)
                    copy_half(kind, n, 1, engine)
            if 0 <= i - 1 < nstep and not by_scalar(i - 1):
                regroup(i - 1)
            if 0 <= i - 3 < nstep:
                add_b2(i - 3)
                store_y(i - 3)
            if 0 <= i - 1 < nstep:
                quantise_h1(i - 1)
            for kind, n, pool, i_transpose, i_quantise in later:
                if i == i_quantise:
                    quantise_halves(kind, n, 0, 2)
            if 0 <= i - 3 < nstep:
                add_gated(i - 3)
                if steps[i - 3][3] == NEXP - 1:
                    store_q(i - 3)
